import numpy as np
import ml_dtypes


def mxq(x, axis, fmt="e4m3"):
    dtype, down = {"e4m3": (ml_dtypes.float8_e4m3fn, 7), "e5m2": (ml_dtypes.float8_e5m2, 14)}[fmt]
    v = np.moveaxis(np.asarray(x, np.float32).astype(ml_dtypes.bfloat16).astype(np.float64), axis, -1)
    blocks = v.reshape(v.shape[:-1] + (-1, 32))
    amax = np.abs(blocks).max(-1, keepdims=True)
    byte = np.maximum(np.where(amax > 0, np.frexp(amax)[1] - 1 + 127, 0) - down, 1)
    scale = np.exp2(byte - 127.0)
    codes = (blocks / scale).astype(np.float32).astype(dtype).astype(np.float64)
    return np.moveaxis((codes * scale).reshape(v.shape), -1, axis)


WIDE = False


def mx_kscale(k):
    if not WIDE:
        return np.ones(k)
    levels = np.array([10, -10, 5, -5, 0])
    a = np.random.permutation(np.resize(levels, k // 512 * 4)).reshape(k // 512, 4)
    idx = np.arange(k)
    return np.exp2(a[idx // 512, idx % 128 // 32])


BF16 = ml_dtypes.bfloat16


def bf(x):
    return np.asarray(x, np.float32).astype(BF16)


def f64(x):
    return np.asarray(x).astype(np.float64)


B, N, VF_D, HID_D, EMB_D = 4096, 128, 512, 512, 128
C = 6.0 / np.sqrt(EMB_D)


def _partial_order_sim(hypers, hypos):
    act = np.maximum(hypers - hypos, 0.0)
    return -np.sqrt(np.sum(act * act, axis=-1))


def setup_inputs():
    s, t = mx_kscale(VF_D), mx_kscale(HID_D)
    return {"vfs": bf(np.random.standard_normal((B, VF_D)) * s),
            "p_lfs": bf(np.random.standard_normal((B, EMB_D)) * 2.0 * C),
            "n_lfs": bf(np.random.standard_normal((N, EMB_D)) * C),
            "W_hidden": bf(np.random.standard_normal((HID_D, VF_D)) / np.sqrt(VF_D) / s[None, :] * t[:, None]),
            "b_hidden": bf(np.random.standard_normal(HID_D) * 0.5 * t),
            "W_embed": bf(np.random.standard_normal((EMB_D, HID_D)) * C / np.sqrt(HID_D) / t[None, :]),
            "b_embed": bf(np.random.standard_normal(EMB_D) * 0.5 * C)}


def reference(vfs, p_lfs, n_lfs, W_hidden, b_hidden, W_embed, b_embed):
    vf_hidden = (mxq(f64(vfs), 1, "e4m3") @ mxq(f64(W_hidden), 1, "e4m3").T) + f64(b_hidden)
    vf_emb = (mxq(vf_hidden, 1, "e4m3") @ mxq(f64(W_embed), 1, "e4m3").T) + f64(b_embed)
    p_scores = _partial_order_sim(f64(p_lfs), vf_emb)
    n_scores = np.stack([_partial_order_sim(nl[None, :], vf_emb) for nl in f64(n_lfs)], axis=1)
    return np.concatenate([p_scores[:, None], n_scores], axis=1)

@@ -1,0 +1,295 @@
+from contextlib import ExitStack
+
+import concourse.masks as masks
+import concourse.mybir as mybir
+
+F32 = mybir.dt.float32
+BF16 = mybir.dt.bfloat16
+U32 = mybir.dt.uint32
+U8 = mybir.dt.uint8
+FP8X4 = mybir.dt.float8_e4m3fn_x4
+ALU = mybir.AluOpType
+ACT = mybir.ActivationFunctionType
+AX = mybir.AxisListType
+
+P = 128
+B = 4096
+NT = B // P
+VF = 512
+HID = 512
+EMB = 128
+NNEG = 128
+CH = 512
+NCH = B // CH
+WG = 1024
+NG = B // WG
+TG = WG // P
+BPU = WG // CH
+JS = 85
+NV = NNEG - JS
+LEAD = 4
+LAG_V = 2
+DEFER = 8
+
+FLOPS = 2 * B * VF * HID + 2 * B * HID * EMB + 4 * B * (NNEG + 1) * EMB
+
+
+def bank_steps():
+    steps = []
+    n_s = (JS + 1) * BPU
+    n_v = NV * BPU
+    total = n_s + n_v
+    for g in range(NG):
+        done_s = 0
+        done_v = 0
+        for k in range(total):
+            if (done_v + 1) * total <= (k + 1) * n_v:
+                steps.append((g, "v", done_v // BPU, done_v % BPU))
+                done_v += 1
+            else:
+                steps.append((g, "s", done_s // BPU, done_s % BPU))
+                done_s += 1
+    return steps
+
+
+def tile_hypernymvisual_acc_t_kernel(tc, vfs, p_lfs, n_lfs, W_hidden, b_hidden, W_embed, b_embed, out):
+    nc = tc.nc
+    with ExitStack() as ctx:
+        keep = ctx.enter_context(tc.tile_pool(name="keep", bufs=1))
+        ident_f = keep.tile([P, P], F32, name="ident_f")
+        masks.make_identity(nc, ident_f[:])
+        ident_b = keep.tile([P, P], BF16, name="ident_b")
+        masks.make_identity(nc, ident_b[:])
+        eT = keep.tile([P, B], F32, name="eT")
+        rp = keep.tile([P, B], F32, name="rp")
+        nT = keep.tile([P, NNEG], F32, name="nT")
+        bias = keep.tile([P, 8], F32, name="bias")
+        warm = keep.tile([P, 2], F32, name="warm")
+        nc.vector.memset(warm[:], 1.0)
+        nc.scalar.activation(out=warm[:, 1:2], in_=warm[:, 0:1], func=ACT.Sqrt)
+
+        fr = ctx.enter_context(tc.tile_pool(name="front", bufs=1))
+        stg = ctx.enter_context(tc.tile_pool(name="stage", bufs=2))
+        with tc.psum_pool(name="fps", bufs=1) as fps:
+            wh_sb = fr.tile([P, 4 * VF], BF16, name="wh_sb")
+            nc.sync.dma_start(
+                out=wh_sb[:].rearrange("p (m k) -> p m k", m=4),
+                in_=W_hidden.rearrange("(m p) k -> p m k", p=P),
+            )
+            x_sb = fr.tile([P, NT * VF], BF16, name="x_sb")
+            x_view = vfs.rearrange("(p t) k -> p (t k)", t=NT)
+            step = NT * VF // 4
+            nc.sync.dma_start(out=x_sb[:, 0:step], in_=x_view[:, 0:step])
+            we_sb = fr.tile([P, HID], BF16, name="we_sb")
+            nc.sync.dma_start(out=we_sb[:], in_=W_embed)
+            n_sb = fr.tile([P, EMB], BF16, name="n_sb")
+            nc.sync.dma_start(out=n_sb[:], in_=n_lfs)
+            zb = fr.tile([P, P], BF16, name="zb")
+            nc.vector.memset(zb[:], 0.0)
+            nc.sync.dma_start(out=zb[0:4, :], in_=b_hidden.rearrange("(m p) -> m p", p=P))
+            nc.sync.dma_start(out=zb[4:5, :], in_=b_embed.rearrange("(o p) -> o p", o=1))
+            for c in range(1, 4):
+                nc.sync.dma_start(out=x_sb[:, c * step:(c + 1) * step], in_=x_view[:, c * step:(c + 1) * step])
+            p_sb = fr.tile([P, NT * EMB], BF16, name="p_sb")
+            nc.sync.dma_start(out=p_sb[:], in_=p_lfs.rearrange("(p t) d -> p (t d)", t=NT))
+
+            x_codes = fr.tile([P, B], U32, name="x_codes", align_bytes=64)
+            x_scales = fr.tile([P, B], U8, name="x_scales", align_bytes=64)
+            wh_codes = fr.tile([P, HID], U32, name="wh_codes", align_bytes=64)
+            wh_scales = fr.tile([P, HID], U8, name="wh_scales", align_bytes=64)
+            we_codes = fr.tile([P, EMB], U32, name="we_codes", align_bytes=64)
+            we_scales = fr.tile([P, EMB], U8, name="we_scales", align_bytes=64)
+
+            def words_to_codes(src_words, first, codes, scales, flip):
+                g = stg.tile([P, 4 * CH], BF16, name="g", tag="g", align_bytes=64)
+                gw = g[:].bitcast(F32)
+                for half in range(2):
+                    tp = fps.tile([P, CH], F32, name="tp", tag="tp", bufs=3)
+                    for tt in range(2):
+                        for u in range(2):
+                            blk = (first + 2 * half + tt) * 256 + 128 * u
+                            nc.tensor.transpose(
+                                tp[:, (2 * tt + u) * P:(2 * tt + u + 1) * P],
+                                src_words[:, blk:blk + P],
+                                ident_f[:],
+                            )
+                    dst = gw[:, half * CH:(half + 1) * CH].rearrange("q (tt c u) -> q tt c u", tt=2, u=2)
+                    src = tp[:].rearrange("q (tt u c) -> q tt c u", tt=2, u=2)
+                    if (half + flip) % 2 == 0:
+                        nc.vector.tensor_copy(out=dst, in_=src)
+                    else:
+                        nc.scalar.copy(out=dst, in_=src)
+                nc.vector.quantize_mx(out=codes.bitcast(FP8X4), scales=scales, in_=g[:])
+
+            words_to_codes(wh_sb[:].bitcast(F32), 0, wh_codes[:], wh_scales[:], 0)
+            xw = x_sb[:].bitcast(F32)
+            for n in range(NCH):
+                words_to_codes(xw, 4 * n, x_codes[:, n * CH:(n + 1) * CH], x_scales[:, n * CH:(n + 1) * CH], n)
+
+            tb = fps.tile([P, CH], BF16, name="tb", tag="tp", bufs=3)
+            for t in range(4):
+                nc.tensor.transpose(tb[:, t * P:(t + 1) * P], we_sb[:, t * P:(t + 1) * P], ident_b[:])
+            g_we = fr.tile([P, EMB, 4], BF16, name="g_we", align_bytes=64)
+            nc.vector.tensor_copy(out=g_we[:], in_=tb[:].rearrange("p (t d) -> p d t", t=4))
+            nc.vector.quantize_mx(out=we_codes[:].bitcast(FP8X4), scales=we_scales[:], in_=g_we[:].rearrange("p d t -> p (d t)"))
+
+            tn = fps.tile([P, CH], BF16, name="tn", tag="tp", bufs=3)
+            nc.tensor.transpose(tn[:, 0:P], n_sb[:], ident_b[:])
+            nc.tensor.transpose(tn[:, P:2 * P], zb[:], ident_b[:])
+            nc.vector.tensor_copy(out=nT[:], in_=tn[:, 0:P])
+            nc.vector.tensor_copy(out=bias[:, 0:5], in_=tn[:, P:P + 5])
+
+            for n in range(NCH):
+                cols = slice(n * CH, (n + 1) * CH)
+                hb = stg.tile([P, 4, CH], BF16, name="hb", tag="hb")
+                for m in range(4):
+                    ph = fps.tile([P, CH], F32, name="ph", tag="ph", bufs=4)
+                    nc.tensor.matmul_mx(
+                        out=ph[:],
+                        lhsT=wh_codes[:, m * P:(m + 1) * P].bitcast(FP8X4),
+                        lhsT_scale=wh_scales[:, m * P:(m + 1) * P],
+                        rhs=x_codes[:, cols].bitcast(FP8X4),
+                        rhs_scale=x_scales[:, cols],
+                        start=True,
+                        stop=True,
+                    )
+                    if m % 2 == 0:
+                        nc.scalar.activation(out=hb[:, m, :], in_=ph[:], func=ACT.Identity, bias=bias[:, m:m + 1])
+                    else:
+                        nc.vector.tensor_scalar(out=hb[:, m, :], in0=ph[:], scalar1=bias[:, m:m + 1], scalar2=None, op0=ALU.add)
+                g2 = stg.tile([P, CH, 4], BF16, name="g2", tag="g2", align_bytes=64)
+                nc.vector.tensor_copy(
+                    out=g2[:].rearrange("p (c i) t -> p c t i", i=4),
+                    in_=hb[:].rearrange("p t (c i) -> p c t i", i=4),
+                )
+                h_codes = stg.tile([P, CH], U32, name="h_codes", tag="h_codes", align_bytes=64)
+                h_scales = stg.tile([P, CH], U8, name="h_scales", tag="h_scales", align_bytes=64)
+                nc.vector.quantize_mx(out=h_codes[:].bitcast(FP8X4), scales=h_scales[:], in_=g2[:].rearrange("p c t -> p (c t)"))
+                pe = fps.tile([P, CH], F32, name="pe", tag="pe", bufs=1)
+                nc.tensor.matmul_mx(
+                    out=pe[:],
+                    lhsT=we_codes[:].bitcast(FP8X4),
+                    lhsT_scale=we_scales[:],
+                    rhs=h_codes[:].bitcast(FP8X4),
+                    rhs_scale=h_scales[:],
+                    start=True,
+                    stop=True,
+                )
+                nc.scalar.activation(out=eT[:, cols], in_=pe[:], func=ACT.Identity, bias=bias[:, 4:5])
+
+            for n in range(NCH):
+                cols = slice(n * CH, (n + 1) * CH)
+                tq = fps.tile([P, CH], BF16, name="tq", tag="tp", bufs=3)
+                for s in range(4):
+                    t = 4 * n + s
+                    nc.tensor.transpose(tq[:, s * P:(s + 1) * P], p_sb[:, t * EMB:(t + 1) * EMB], ident_b[:])
+                nc.vector.tensor_tensor(out=rp[:, cols], in0=eT[:, cols], in1=tq[:], op=ALU.subtract)
+            nc.vector.tensor_scalar_min(out=rp[:], in0=rp[:], scalar1=0.0)
+
+        acc = ctx.enter_context(tc.tile_pool(name="acc", bufs=2))
+        rpool = ctx.enter_context(tc.tile_pool(name="rpool", bufs=6))
+        banks = ctx.enter_context(tc.psum_pool(name="banks", bufs=8))
+        junk = keep.tile([P, P], F32, name="junk")
+        out_view = out.rearrange("(p t) c -> p (t c)", t=NT)
+        steps = bank_steps()
+        n_steps = len(steps)
+        per_group = n_steps // NG
+        diffs = {}
+        filled = {}
+        sums = {}
+        late = {}
+
+        def write_diff(k):
+            g, kind, u, q = steps[k]
+            if q != 0:
+                return
+            if kind == "s" and u == JS:
+                diffs[(g, kind, u)] = rp[:, g * WG:(g + 1) * WG]
+                return
+            j = u if kind == "s" else JS + u
+            rt = rpool.tile([P, WG], F32, name="rt", tag="rt")
+            nc.vector.tensor_scalar(
+                out=rt[:],
+                in0=eT[:, g * WG:(g + 1) * WG],
+                scalar1=nT[:, j:j + 1],
+                scalar2=0.0,
+                op0=ALU.subtract,
+                op1=ALU.min,
+            )
+            diffs[(g, kind, u)] = rt[:]
+
+        def transpose_bank(k):
+            g, kind, u, q = steps[k]
+            r = diffs[(g, kind, u)]
+            bank = banks.tile([P, CH], F32, name="bank", tag="bank")
+            for s in range(4):
+                nc.tensor.transpose(bank[:, s * P:(s + 1) * P], r[:, q * CH + s * P:q * CH + (s + 1) * P], ident_f[:])
+            filled[k] = bank
+
+        def consume(k):
+            g, kind, u, q = steps[k]
+            if g not in sums:
+                sum_s = acc.tile([P, TG, JS + 1], F32, name="sum_s", tag="sum_s")
+                stats = acc.tile([P, NV * TG, 6], F32, name="stats", tag="stats")
+                sums[g] = (sum_s, stats)
+            sum_s, stats = sums[g]
+            bank = filled[k]
+            for s in range(4):
+                t = 4 * q + s
+                if kind == "s":
+                    col = 0 if u == JS else u + 1
+                    nc.scalar.activation(out=junk[:], in_=bank[:, s * P:(s + 1) * P], func=ACT.Square, accum_out=sum_s[:, t, col:col + 1])
+                else:
+                    nc.vector.bn_stats(out=stats[:, u * TG + t, :], in_=bank[:, s * P:(s + 1) * P])
+
+        def finish_sums(g):
+            sum_s, stats = sums[g]
+            st = stats[:].rearrange("p n (h s) -> p (n h) s", h=2)
+            msq = acc.tile([P, NV * TG * 2], F32, name="msq", tag="msq")
+            nc.vector.tensor_tensor(out=msq[:], in0=st[:, :, 1], in1=st[:, :, 1], op=ALU.mult)
+            nc.vector.scalar_tensor_tensor(out=msq[:], in0=msq[:], scalar=float(EMB // 2), in1=st[:, :, 2], op0=ALU.mult, op1=ALU.add)
+            sum_v = acc.tile([P, NV * TG], F32, name="sum_v", tag="sum_v")
+            nc.vector.tensor_reduce(out=sum_v[:], in_=msq[:].rearrange("p (n h) -> p n h", h=2), axis=AX.X, op=ALU.add)
+            late[g] = sum_v
+
+        def finish_roots(g):
+            sum_s, stats = sums[g]
+            sum_v = late[g]
+            root = acc.tile([P, TG, NNEG + 1], F32, name="root", tag="root")
+            nc.scalar.activation(out=root[:, :, 0:JS + 1], in_=sum_s[:], func=ACT.Sqrt)
+            nc.scalar.activation(out=root[:, :, JS + 1:NNEG + 1], in_=sum_v[:].rearrange("p (v t) -> p t v", t=TG), func=ACT.Sqrt)
+            late[g] = root
+
+        def finish_store(g):
+            root = late[g]
+            res = acc.tile([P, TG * (NNEG + 1)], F32, name="res", tag="res")
+            nc.vector.tensor_scalar(out=res[:], in0=root[:].rearrange("p t c -> p (t c)"), scalar1=-1.0, scalar2=None, op0=ALU.mult)
+            width = TG * (NNEG + 1)
+            nc.sync.dma_start(out=out_view[:, g * width:(g + 1) * width], in_=res[:])
+
+        with tc.manual_schedule():
+            pending_v = []
+            for k in range(n_steps + LEAD):
+                if k < n_steps:
+                    write_diff(k)
+                b = k - LEAD
+                if b < 0:
+                    continue
+                transpose_bank(b)
+                if steps[b][1] == "s":
+                    consume(b)
+                else:
+                    pending_v.append(b)
+                last_of_group = (b + 1) % per_group == 0
+                while pending_v and (pending_v[0] <= b - LAG_V or last_of_group):
+                    consume(pending_v[0])
+                    pending_v = pending_v[1:]
+                g_now = steps[b][0]
+                if last_of_group:
+                    finish_sums(g_now)
+                if g_now > 0 and b % per_group == DEFER:
+                    finish_roots(g_now - 1)
+                if g_now > 0 and b % per_group == 2 * DEFER:
+                    finish_store(g_now - 1)
+            finish_roots(NG - 1)
+            finish_store(NG - 1)

@@ -29,6 +29,7 @@ JS = 85
 NV = NNEG - JS
 LEAD = 4
 LAG_V = 2
+NJUNK = 8
 DEFER = 8
 
 FLOPS = 2 * B * VF * HID + 2 * B * HID * EMB + 4 * B * (NNEG + 1) * EMB
@@ -189,7 +190,7 @@ def tile_hypernymvisual_acc_t_kernel(tc, vfs, p_lfs, n_lfs, W_hidden, b_hidden, 
         acc = ctx.enter_context(tc.tile_pool(name="acc", bufs=2))
         rpool = ctx.enter_context(tc.tile_pool(name="rpool", bufs=6))
         banks = ctx.enter_context(tc.psum_pool(name="banks", bufs=8))
-        junk = keep.tile([P, P], F32, name="junk")
+        junk = keep.tile([P, NJUNK, P], F32, name="junk")
         out_view = out.rearrange("(p t) c -> p (t c)", t=NT)
         steps = bank_steps()
         n_steps = len(steps)
@@ -238,7 +239,7 @@ def tile_hypernymvisual_acc_t_kernel(tc, vfs, p_lfs, n_lfs, W_hidden, b_hidden, 
                 t = 4 * q + s
                 if kind == "s":
                     col = 0 if u == JS else u + 1
-                    nc.scalar.activation(out=junk[:], in_=bank[:, s * P:(s + 1) * P], func=ACT.Square, accum_out=sum_s[:, t, col:col + 1])
+                    nc.scalar.activation(out=junk[:, (4 * k + s) % NJUNK, :], in_=bank[:, s * P:(s + 1) * P], func=ACT.Square, accum_out=sum_s[:, t, col:col + 1])
                 else:
                     nc.vector.bn_stats(out=stats[:, u * TG + t, :], in_=bank[:, s * P:(s + 1) * P])
 

@@ -25,7 +25,7 @@ WG = 1024
 NG = B // WG
 TG = WG // P
 BPU = WG // CH
-JS = 85
+JS = 78
 NV = NNEG - JS
 LEAD = 4
 LAG_V = 2

@@ -25,7 +25,7 @@ WG = 1024
 NG = B // WG
 TG = WG // P
 BPU = WG // CH
-JS = 78
+JS = 92
 NV = NNEG - JS
 LEAD = 4
 LAG_V = 2

@@ -21,36 +21,14 @@ EMB = 128
 NNEG = 128
 CH = 512
 NCH = B // CH
-WG = 1024
-NG = B // WG
-TG = WG // P
-BPU = WG // CH
-JS = 92
-NV = NNEG - JS
-LEAD = 4
-LAG_V = 2
-NJUNK = 8
-DEFER = 8
+DC = 16
+NDC = EMB // DC
+NCHUNK = NT * NDC
+VSQ = 38
+LEAD = 3
+TG = 8
 
 FLOPS = 2 * B * VF * HID + 2 * B * HID * EMB + 4 * B * (NNEG + 1) * EMB
-
-
-def bank_steps():
-    steps = []
-    n_s = (JS + 1) * BPU
-    n_v = NV * BPU
-    total = n_s + n_v
-    for g in range(NG):
-        done_s = 0
-        done_v = 0
-        for k in range(total):
-            if (done_v + 1) * total <= (k + 1) * n_v:
-                steps.append((g, "v", done_v // BPU, done_v % BPU))
-                done_v += 1
-            else:
-                steps.append((g, "s", done_s // BPU, done_s % BPU))
-                done_s += 1
-    return steps
 
 
 def tile_hypernymvisual_acc_t_kernel(tc, vfs, p_lfs, n_lfs, W_hidden, b_hidden, W_embed, b_embed, out):
@@ -61,17 +39,15 @@ def tile_hypernymvisual_acc_t_kernel(tc, vfs, p_lfs, n_lfs, W_hidden, b_hidden, 
         masks.make_identity(nc, ident_f[:])
         ident_b = keep.tile([P, P], BF16, name="ident_b")
         masks.make_identity(nc, ident_b[:])
-        eT = keep.tile([P, B], F32, name="eT")
-        rp = keep.tile([P, B], F32, name="rp")
-        nT = keep.tile([P, NNEG], F32, name="nT")
+        emb = keep.tile([P, NT, EMB], F32, name="emb")
+        n_bc = keep.tile([P, EMB, NNEG], F32, name="n_bc")
+        res = keep.tile([P, NT, NNEG + 1], F32, name="res")
         bias = keep.tile([P, 8], F32, name="bias")
         warm = keep.tile([P, 2], F32, name="warm")
         nc.vector.memset(warm[:], 1.0)
         nc.scalar.activation(out=warm[:, 1:2], in_=warm[:, 0:1], func=ACT.Sqrt)
 
-        fr = ctx.enter_context(tc.tile_pool(name="front", bufs=1))
-        stg = ctx.enter_context(tc.tile_pool(name="stage", bufs=2))
-        with tc.psum_pool(name="fps", bufs=1) as fps:
+        with tc.tile_pool(name="front", bufs=1) as fr, tc.tile_pool(name="stage", bufs=2) as stg, tc.psum_pool(name="fps", bufs=1) as fps:
             wh_sb = fr.tile([P, 4 * VF], BF16, name="wh_sb")
             nc.sync.dma_start(
                 out=wh_sb[:].rearrange("p (m k) -> p m k", m=4),
@@ -83,25 +59,33 @@ def tile_hypernymvisual_acc_t_kernel(tc, vfs, p_lfs, n_lfs, W_hidden, b_hidden, 
             nc.sync.dma_start(out=x_sb[:, 0:step], in_=x_view[:, 0:step])
             we_sb = fr.tile([P, HID], BF16, name="we_sb")
             nc.sync.dma_start(out=we_sb[:], in_=W_embed)
-            n_sb = fr.tile([P, EMB], BF16, name="n_sb")
-            nc.sync.dma_start(out=n_sb[:], in_=n_lfs)
             zb = fr.tile([P, P], BF16, name="zb")
             nc.vector.memset(zb[:], 0.0)
             nc.sync.dma_start(out=zb[0:4, :], in_=b_hidden.rearrange("(m p) -> m p", p=P))
-            nc.sync.dma_start(out=zb[4:5, :], in_=b_embed.rearrange("(o p) -> o p", o=1))
+            b_bc = fr.tile([P, EMB], BF16, name="b_bc")
+            nc.sync.dma_start(out=b_bc[:], in_=b_embed.partition_broadcast(P))
+            nb16 = fr.tile([P, NNEG * EMB], BF16, name="nb16")
+            nc.sync.dma_start(out=nb16[:], in_=n_lfs.rearrange("j d -> (j d)").partition_broadcast(P))
             for c in range(1, 4):
                 nc.sync.dma_start(out=x_sb[:, c * step:(c + 1) * step], in_=x_view[:, c * step:(c + 1) * step])
-            p_sb = fr.tile([P, NT * EMB], BF16, name="p_sb")
-            nc.sync.dma_start(out=p_sb[:], in_=p_lfs.rearrange("(p t) d -> p (t d)", t=NT))
 
-            x_codes = fr.tile([P, B], U32, name="x_codes", align_bytes=64)
-            x_scales = fr.tile([P, B], U8, name="x_scales", align_bytes=64)
+            nb_view = nb16[:].rearrange("p (j d) -> p d j", d=EMB)
+            for c in range(16):
+                nc.gpsimd.tensor_scalar(
+                    out=n_bc[:, 8 * c:8 * c + 8, :],
+                    in0=nb_view[:, 8 * c:8 * c + 8, :],
+                    scalar1=1.0,
+                    scalar2=0.0,
+                    op0=ALU.mult,
+                    op1=ALU.add,
+                )
+
             wh_codes = fr.tile([P, HID], U32, name="wh_codes", align_bytes=64)
             wh_scales = fr.tile([P, HID], U8, name="wh_scales", align_bytes=64)
             we_codes = fr.tile([P, EMB], U32, name="we_codes", align_bytes=64)
             we_scales = fr.tile([P, EMB], U8, name="we_scales", align_bytes=64)
 
-            def words_to_codes(src_words, first, codes, scales, flip):
+            def words_to_codes(src_words, first, codes, scales):
                 g = stg.tile([P, 4 * CH], BF16, name="g", tag="g", align_bytes=64)
                 gw = g[:].bitcast(F32)
                 for half in range(2):
@@ -116,16 +100,10 @@ def tile_hypernymvisual_acc_t_kernel(tc, vfs, p_lfs, n_lfs, W_hidden, b_hidden, 
                             )
                     dst = gw[:, half * CH:(half + 1) * CH].rearrange("q (tt c u) -> q tt c u", tt=2, u=2)
                     src = tp[:].rearrange("q (tt u c) -> q tt c u", tt=2, u=2)
-                    if (half + flip) % 2 == 0:
-                        nc.vector.tensor_copy(out=dst, in_=src)
-                    else:
-                        nc.scalar.copy(out=dst, in_=src)
+                    nc.scalar.copy(out=dst, in_=src)
                 nc.vector.quantize_mx(out=codes.bitcast(FP8X4), scales=scales, in_=g[:])
 
-            words_to_codes(wh_sb[:].bitcast(F32), 0, wh_codes[:], wh_scales[:], 0)
-            xw = x_sb[:].bitcast(F32)
-            for n in range(NCH):
-                words_to_codes(xw, 4 * n, x_codes[:, n * CH:(n + 1) * CH], x_scales[:, n * CH:(n + 1) * CH], n)
+            words_to_codes(wh_sb[:].bitcast(F32), 0, wh_codes[:], wh_scales[:])
 
             tb = fps.tile([P, CH], BF16, name="tb", tag="tp", bufs=3)
             for t in range(4):
@@ -135,13 +113,14 @@ def tile_hypernymvisual_acc_t_kernel(tc, vfs, p_lfs, n_lfs, W_hidden, b_hidden, 
             nc.vector.quantize_mx(out=we_codes[:].bitcast(FP8X4), scales=we_scales[:], in_=g_we[:].rearrange("p d t -> p (d t)"))
 
             tn = fps.tile([P, CH], BF16, name="tn", tag="tp", bufs=3)
-            nc.tensor.transpose(tn[:, 0:P], n_sb[:], ident_b[:])
-            nc.tensor.transpose(tn[:, P:2 * P], zb[:], ident_b[:])
-            nc.vector.tensor_copy(out=nT[:], in_=tn[:, 0:P])
-            nc.vector.tensor_copy(out=bias[:, 0:5], in_=tn[:, P:P + 5])
+            nc.tensor.transpose(tn[:, 0:P], zb[:], ident_b[:])
+            nc.vector.tensor_copy(out=bias[:, 0:4], in_=tn[:, 0:4])
 
+            xw = x_sb[:].bitcast(F32)
             for n in range(NCH):
-                cols = slice(n * CH, (n + 1) * CH)
+                x_codes = stg.tile([P, CH], U32, name="x_codes", tag="x_codes", align_bytes=64)
+                x_scales = stg.tile([P, CH], U8, name="x_scales", tag="x_scales", align_bytes=64)
+                words_to_codes(xw, 4 * n, x_codes[:], x_scales[:])
                 hb = stg.tile([P, 4, CH], BF16, name="hb", tag="hb")
                 for m in range(4):
                     ph = fps.tile([P, CH], F32, name="ph", tag="ph", bufs=4)
@@ -149,15 +128,12 @@ def tile_hypernymvisual_acc_t_kernel(tc, vfs, p_lfs, n_lfs, W_hidden, b_hidden, 
                         out=ph[:],
                         lhsT=wh_codes[:, m * P:(m + 1) * P].bitcast(FP8X4),
                         lhsT_scale=wh_scales[:, m * P:(m + 1) * P],
-                        rhs=x_codes[:, cols].bitcast(FP8X4),
-                        rhs_scale=x_scales[:, cols],
+                        rhs=x_codes[:].bitcast(FP8X4),
+                        rhs_scale=x_scales[:],
                         start=True,
                         stop=True,
                     )
-                    if m % 2 == 0:
-                        nc.scalar.activation(out=hb[:, m, :], in_=ph[:], func=ACT.Identity, bias=bias[:, m:m + 1])
-                    else:
-                        nc.vector.tensor_scalar(out=hb[:, m, :], in0=ph[:], scalar1=bias[:, m:m + 1], scalar2=None, op0=ALU.add)
+                    nc.scalar.activation(out=hb[:, m, :], in_=ph[:], func=ACT.Identity, bias=bias[:, m:m + 1])
                 g2 = stg.tile([P, CH, 4], BF16, name="g2", tag="g2", align_bytes=64)
                 nc.vector.tensor_copy(
                     out=g2[:].rearrange("p (c i) t -> p c t i", i=4),
@@ -166,131 +142,129 @@ def tile_hypernymvisual_acc_t_kernel(tc, vfs, p_lfs, n_lfs, W_hidden, b_hidden, 
                 h_codes = stg.tile([P, CH], U32, name="h_codes", tag="h_codes", align_bytes=64)
                 h_scales = stg.tile([P, CH], U8, name="h_scales", tag="h_scales", align_bytes=64)
                 nc.vector.quantize_mx(out=h_codes[:].bitcast(FP8X4), scales=h_scales[:], in_=g2[:].rearrange("p c t -> p (c t)"))
-                pe = fps.tile([P, CH], F32, name="pe", tag="pe", bufs=1)
-                nc.tensor.matmul_mx(
-                    out=pe[:],
-                    lhsT=we_codes[:].bitcast(FP8X4),
-                    lhsT_scale=we_scales[:],
-                    rhs=h_codes[:].bitcast(FP8X4),
-                    rhs_scale=h_scales[:],
-                    start=True,
-                    stop=True,
-                )
-                nc.scalar.activation(out=eT[:, cols], in_=pe[:], func=ACT.Identity, bias=bias[:, 4:5])
-
-            for n in range(NCH):
-                cols = slice(n * CH, (n + 1) * CH)
-                tq = fps.tile([P, CH], BF16, name="tq", tag="tp", bufs=3)
+                pe = fps.tile([P, 4, EMB], F32, name="pe", tag="pe", bufs=1)
                 for s in range(4):
-                    t = 4 * n + s
-                    nc.tensor.transpose(tq[:, s * P:(s + 1) * P], p_sb[:, t * EMB:(t + 1) * EMB], ident_b[:])
-                nc.vector.tensor_tensor(out=rp[:, cols], in0=eT[:, cols], in1=tq[:], op=ALU.subtract)
-            nc.vector.tensor_scalar_min(out=rp[:], in0=rp[:], scalar1=0.0)
+                    nc.tensor.matmul_mx(
+                        out=pe[:, s, :],
+                        lhsT=h_codes[:, s * P:(s + 1) * P].bitcast(FP8X4),
+                        lhsT_scale=h_scales[:, s * P:(s + 1) * P],
+                        rhs=we_codes[:].bitcast(FP8X4),
+                        rhs_scale=we_scales[:],
+                        start=True,
+                        stop=True,
+                    )
+                nc.vector.tensor_tensor(
+                    out=emb[:, 4 * n:4 * n + 4, :],
+                    in0=pe[:],
+                    in1=b_bc[:].unsqueeze(1).to_broadcast([P, 4, EMB]),
+                    op=ALU.add,
+                )
 
-        acc = ctx.enter_context(tc.tile_pool(name="acc", bufs=2))
         rpool = ctx.enter_context(tc.tile_pool(name="rpool", bufs=6))
-        banks = ctx.enter_context(tc.psum_pool(name="banks", bufs=8))
-        junk = keep.tile([P, NJUNK, P], F32, name="junk")
+        small = ctx.enter_context(tc.tile_pool(name="small", bufs=3))
+        accs = ctx.enter_context(tc.psum_pool(name="accs", bufs=3))
+        backs = ctx.enter_context(tc.psum_pool(name="backs", bufs=2))
         out_view = out.rearrange("(p t) c -> p (t c)", t=NT)
-        steps = bank_steps()
-        n_steps = len(steps)
-        per_group = n_steps // NG
+        pos = ctx.enter_context(tc.tile_pool(name="pos", bufs=1))
+        p_sb = pos.tile([P, NT, EMB], BF16, name="p_sb")
+        nc.sync.dma_start(out=p_sb[:].rearrange("p t d -> p (t d)"), in_=p_lfs.rearrange("(p t) d -> p (t d)", t=NT))
+        xp = pos.tile([P, NT, EMB], F32, name="xp")
+        sum_p = pos.tile([P, NT], F32, name="sum_p")
+
+        def positives(g, stage):
+            ts = slice(g * TG, (g + 1) * TG)
+            if stage == 0:
+                nc.vector.tensor_tensor(out=xp[:, ts, :], in0=p_sb[:, ts, :], in1=emb[:, ts, :], op=ALU.subtract)
+                nc.vector.tensor_scalar_max(out=xp[:, ts, :], in0=xp[:, ts, :], scalar1=0.0)
+            elif stage == 1:
+                nc.scalar.activation(out=xp[:, ts, :], in_=xp[:, ts, :], func=ACT.Square)
+            elif stage == 2:
+                nc.vector.tensor_reduce(out=sum_p[:, ts], in_=xp[:, ts, :], axis=AX.X, op=ALU.add)
+            elif stage == 3:
+                nc.scalar.activation(out=sum_p[:, ts], in_=sum_p[:, ts], func=ACT.Sqrt)
+            else:
+                nc.vector.tensor_scalar(out=res[:, ts, 0], in0=sum_p[:, ts], scalar1=-1.0, scalar2=None, op0=ALU.mult)
         diffs = {}
-        filled = {}
-        sums = {}
-        late = {}
+        open_acc = {}
 
-        def write_diff(k):
-            g, kind, u, q = steps[k]
-            if q != 0:
-                return
-            if kind == "s" and u == JS:
-                diffs[(g, kind, u)] = rp[:, g * WG:(g + 1) * WG]
-                return
-            j = u if kind == "s" else JS + u
-            rt = rpool.tile([P, WG], F32, name="rt", tag="rt")
-            nc.vector.tensor_scalar(
-                out=rt[:],
-                in0=eT[:, g * WG:(g + 1) * WG],
-                scalar1=nT[:, j:j + 1],
-                scalar2=0.0,
-                op0=ALU.subtract,
-                op1=ALU.min,
-            )
-            diffs[(g, kind, u)] = rt[:]
+        def write_diffs(c):
+            t = c // NDC
+            rt = rpool.tile([P, DC, NNEG], F32, name="rt", tag="rt")
+            for dd in range(DC):
+                d = (c % NDC) * DC + dd
+                nc.vector.tensor_scalar(
+                    out=rt[:, dd, :],
+                    in0=n_bc[:, d, :],
+                    scalar1=emb[:, t, d:d + 1],
+                    scalar2=0.0,
+                    op0=ALU.subtract,
+                    op1=ALU.max,
+                )
+            diffs[c] = rt
 
-        def transpose_bank(k):
-            g, kind, u, q = steps[k]
-            r = diffs[(g, kind, u)]
-            bank = banks.tile([P, CH], F32, name="bank", tag="bank")
-            for s in range(4):
-                nc.tensor.transpose(bank[:, s * P:(s + 1) * P], r[:, q * CH + s * P:q * CH + (s + 1) * P], ident_f[:])
-            filled[k] = bank
+        def square_and_add(c):
+            t = c // NDC
+            rt = diffs[c]
+            if ((c + 1) * VSQ) // NCHUNK > (c * VSQ) // NCHUNK:
+                nc.vector.tensor_tensor(out=rt[:], in0=rt[:], in1=rt[:], op=ALU.mult)
+            else:
+                nc.scalar.activation(out=rt[:], in_=rt[:], func=ACT.Square)
+            if c % NDC == 0:
+                acc = accs.tile([P, P], F32, name="acc", tag="acc")
+                open_acc[t] = acc
+            acc = open_acc[t]
+            for dd in range(DC):
+                d = (c % NDC) * DC + dd
+                nc.tensor.matmul(
+                    out=acc[:],
+                    lhsT=rt[:, dd, :],
+                    rhs=ident_f[:],
+                    is_transpose=True,
+                    start=(d == 0),
+                    stop=(d == EMB - 1),
+                )
 
-        def consume(k):
-            g, kind, u, q = steps[k]
-            if g not in sums:
-                sum_s = acc.tile([P, TG, JS + 1], F32, name="sum_s", tag="sum_s")
-                stats = acc.tile([P, NV * TG, 6], F32, name="stats", tag="stats")
-                sums[g] = (sum_s, stats)
-            sum_s, stats = sums[g]
-            bank = filled[k]
-            for s in range(4):
-                t = 4 * q + s
-                if kind == "s":
-                    col = 0 if u == JS else u + 1
-                    nc.scalar.activation(out=junk[:, (4 * k + s) % NJUNK, :], in_=bank[:, s * P:(s + 1) * P], func=ACT.Square, accum_out=sum_s[:, t, col:col + 1])
-                else:
-                    nc.vector.bn_stats(out=stats[:, u * TG + t, :], in_=bank[:, s * P:(s + 1) * P])
+        roots = {}
+        backed = {}
 
-        def finish_sums(g):
-            sum_s, stats = sums[g]
-            st = stats[:].rearrange("p n (h s) -> p (n h) s", h=2)
-            msq = acc.tile([P, NV * TG * 2], F32, name="msq", tag="msq")
-            nc.vector.tensor_tensor(out=msq[:], in0=st[:, :, 1], in1=st[:, :, 1], op=ALU.mult)
-            nc.vector.scalar_tensor_tensor(out=msq[:], in0=msq[:], scalar=float(EMB // 2), in1=st[:, :, 2], op0=ALU.mult, op1=ALU.add)
-            sum_v = acc.tile([P, NV * TG], F32, name="sum_v", tag="sum_v")
-            nc.vector.tensor_reduce(out=sum_v[:], in_=msq[:].rearrange("p (n h) -> p n h", h=2), axis=AX.X, op=ALU.add)
-            late[g] = sum_v
+        def finish_root(t):
+            root = small.tile([P, P], F32, name="root", tag="root")
+            nc.scalar.activation(out=root[:], in_=open_acc[t][:], func=ACT.Sqrt)
+            roots[t] = root
 
-        def finish_roots(g):
-            sum_s, stats = sums[g]
-            sum_v = late[g]
-            root = acc.tile([P, TG, NNEG + 1], F32, name="root", tag="root")
-            nc.scalar.activation(out=root[:, :, 0:JS + 1], in_=sum_s[:], func=ACT.Sqrt)
-            nc.scalar.activation(out=root[:, :, JS + 1:NNEG + 1], in_=sum_v[:].rearrange("p (v t) -> p t v", t=TG), func=ACT.Sqrt)
-            late[g] = root
+        def finish_back(t):
+            back = backs.tile([P, P], F32, name="back", tag="back")
+            nc.tensor.transpose(back[:], roots[t][:], ident_f[:])
+            backed[t] = back
 
-        def finish_store(g):
-            root = late[g]
-            res = acc.tile([P, TG * (NNEG + 1)], F32, name="res", tag="res")
-            nc.vector.tensor_scalar(out=res[:], in0=root[:].rearrange("p t c -> p (t c)"), scalar1=-1.0, scalar2=None, op0=ALU.mult)
-            width = TG * (NNEG + 1)
-            nc.sync.dma_start(out=out_view[:, g * width:(g + 1) * width], in_=res[:])
+        def finish_store(t):
+            nc.vector.tensor_scalar(out=res[:, t, 1:NNEG + 1], in0=backed[t][:], scalar1=-1.0, scalar2=None, op0=ALU.mult)
+            if (t + 1) % TG == 0:
+                width = TG * (NNEG + 1)
+                g = t // TG
+                nc.sync.dma_start(
+                    out=out_view[:, g * width:(g + 1) * width],
+                    in_=res[:, g * TG:(g + 1) * TG, :].rearrange("p t c -> p (t c)"),
+                )
 
         with tc.manual_schedule():
-            pending_v = []
-            for k in range(n_steps + LEAD):
-                if k < n_steps:
-                    write_diff(k)
-                b = k - LEAD
-                if b < 0:
+            for k in range(NCHUNK + LEAD):
+                if k < NCHUNK:
+                    write_diffs(k)
+                c = k - LEAD
+                if c < 0:
                     continue
-                transpose_bank(b)
-                if steps[b][1] == "s":
-                    consume(b)
-                else:
-                    pending_v.append(b)
-                last_of_group = (b + 1) % per_group == 0
-                while pending_v and (pending_v[0] <= b - LAG_V or last_of_group):
-                    consume(pending_v[0])
-                    pending_v = pending_v[1:]
-                g_now = steps[b][0]
-                if last_of_group:
-                    finish_sums(g_now)
-                if g_now > 0 and b % per_group == DEFER:
-                    finish_roots(g_now - 1)
-                if g_now > 0 and b % per_group == 2 * DEFER:
-                    finish_store(g_now - 1)
-            finish_roots(NG - 1)
-            finish_store(NG - 1)
+                square_and_add(c)
+                in_group = c % (TG * NDC)
+                if in_group % 4 == 0 and 8 <= in_group < 28:
+                    positives(c // (TG * NDC), (in_group - 8) // 4)
+                if c >= NDC:
+                    if c % NDC == 0:
+                        finish_root(c // NDC - 1)
+                    if c % NDC == 2:
+                        finish_back(c // NDC - 1)
+                    if c % NDC == 5:
+                        finish_store(c // NDC - 1)
+            finish_root(NT - 1)
+            finish_back(NT - 1)
+            finish_store(NT - 1)

@@ -21,11 +21,14 @@ EMB = 128
 NNEG = 128
 CH = 512
 NCH = B // CH
-DC = 16
+DC = 4
 NDC = EMB // DC
-NCHUNK = NT * NDC
-VSQ = 38
-LEAD = 3
+NCHUNK = (NT // 2) * NDC
+VSQ = 70
+LEAD = 4
+FIRST_WARM = 6
+WARM_EVERY = 64
+WARM = 3
 TG = 8
 
 FLOPS = 2 * B * VF * HID + 2 * B * HID * EMB + 4 * B * (NNEG + 1) * EMB
@@ -43,6 +46,10 @@ def tile_hypernymvisual_acc_t_kernel(tc, vfs, p_lfs, n_lfs, W_hidden, b_hidden, 
         n_bc = keep.tile([P, EMB, NNEG], F32, name="n_bc")
         res = keep.tile([P, NT, NNEG + 1], F32, name="res")
         bias = keep.tile([P, 8], F32, name="bias")
+        we_codes = keep.tile([P, EMB], U32, name="we_codes", align_bytes=64)
+        we_scales = keep.tile([P, EMB], U8, name="we_scales", align_bytes=64)
+        last_codes = keep.tile([P, CH], U32, name="last_codes", align_bytes=64)
+        last_scales = keep.tile([P, CH], U8, name="last_scales", align_bytes=64)
         warm = keep.tile([P, 2], F32, name="warm")
         nc.vector.memset(warm[:], 1.0)
         nc.scalar.activation(out=warm[:, 1:2], in_=warm[:, 0:1], func=ACT.Sqrt)
@@ -82,8 +89,6 @@ def tile_hypernymvisual_acc_t_kernel(tc, vfs, p_lfs, n_lfs, W_hidden, b_hidden, 
 
             wh_codes = fr.tile([P, HID], U32, name="wh_codes", align_bytes=64)
             wh_scales = fr.tile([P, HID], U8, name="wh_scales", align_bytes=64)
-            we_codes = fr.tile([P, EMB], U32, name="we_codes", align_bytes=64)
-            we_scales = fr.tile([P, EMB], U8, name="we_scales", align_bytes=64)
 
             def words_to_codes(src_words, first, codes, scales):
                 g = stg.tile([P, 4 * CH], BF16, name="g", tag="g", align_bytes=64)
@@ -139,8 +144,12 @@ def tile_hypernymvisual_acc_t_kernel(tc, vfs, p_lfs, n_lfs, W_hidden, b_hidden, 
                     out=g2[:].rearrange("p (c i) t -> p c t i", i=4),
                     in_=hb[:].rearrange("p t (c i) -> p c t i", i=4),
                 )
-                h_codes = stg.tile([P, CH], U32, name="h_codes", tag="h_codes", align_bytes=64)
-                h_scales = stg.tile([P, CH], U8, name="h_scales", tag="h_scales", align_bytes=64)
+                if n == NCH - 1:
+                    h_codes = last_codes
+                    h_scales = last_scales
+                else:
+                    h_codes = stg.tile([P, CH], U32, name="h_codes", tag="h_codes", align_bytes=64)
+                    h_scales = stg.tile([P, CH], U8, name="h_scales", tag="h_scales", align_bytes=64)
                 nc.vector.quantize_mx(out=h_codes[:].bitcast(FP8X4), scales=h_scales[:], in_=g2[:].rearrange("p c t -> p (c t)"))
                 pe = fps.tile([P, 4, EMB], F32, name="pe", tag="pe", bufs=1)
                 for s in range(4):
@@ -160,10 +169,11 @@ def tile_hypernymvisual_acc_t_kernel(tc, vfs, p_lfs, n_lfs, W_hidden, b_hidden, 
                     op=ALU.add,
                 )
 
-        rpool = ctx.enter_context(tc.tile_pool(name="rpool", bufs=6))
-        small = ctx.enter_context(tc.tile_pool(name="small", bufs=3))
-        accs = ctx.enter_context(tc.psum_pool(name="accs", bufs=3))
+        rpool = ctx.enter_context(tc.tile_pool(name="rpool", bufs=12))
+        small = ctx.enter_context(tc.tile_pool(name="small", bufs=4))
+        accs = ctx.enter_context(tc.psum_pool(name="accs", bufs=4))
         backs = ctx.enter_context(tc.psum_pool(name="backs", bufs=2))
+        idle = ctx.enter_context(tc.psum_pool(name="idle", bufs=2))
         out_view = out.rearrange("(p t) c -> p (t c)", t=NT)
         pos = ctx.enter_context(tc.tile_pool(name="pos", bufs=1))
         p_sb = pos.tile([P, NT, EMB], BF16, name="p_sb")
@@ -188,40 +198,55 @@ def tile_hypernymvisual_acc_t_kernel(tc, vfs, p_lfs, n_lfs, W_hidden, b_hidden, 
         open_acc = {}
 
         def write_diffs(c):
-            t = c // NDC
-            rt = rpool.tile([P, DC, NNEG], F32, name="rt", tag="rt")
-            for dd in range(DC):
-                d = (c % NDC) * DC + dd
-                nc.vector.tensor_scalar(
-                    out=rt[:, dd, :],
-                    in0=n_bc[:, d, :],
-                    scalar1=emb[:, t, d:d + 1],
-                    scalar2=0.0,
-                    op0=ALU.subtract,
-                    op1=ALU.max,
-                )
+            a = c // NDC
+            rt = rpool.tile([P, 2, DC, NNEG], F32, name="rt", tag="rt")
+            for h in range(2):
+                for dd in range(DC):
+                    d = (c % NDC) * DC + dd
+                    nc.vector.tensor_scalar(
+                        out=rt[:, h, dd, :],
+                        in0=n_bc[:, d, :],
+                        scalar1=emb[:, 2 * a + h, d:d + 1],
+                        scalar2=0.0,
+                        op0=ALU.subtract,
+                        op1=ALU.max,
+                    )
             diffs[c] = rt
 
         def square_and_add(c):
-            t = c // NDC
+            a = c // NDC
             rt = diffs[c]
             if ((c + 1) * VSQ) // NCHUNK > (c * VSQ) // NCHUNK:
                 nc.vector.tensor_tensor(out=rt[:], in0=rt[:], in1=rt[:], op=ALU.mult)
             else:
                 nc.scalar.activation(out=rt[:], in_=rt[:], func=ACT.Square)
             if c % NDC == 0:
-                acc = accs.tile([P, P], F32, name="acc", tag="acc")
-                open_acc[t] = acc
-            acc = open_acc[t]
+                for h in range(2):
+                    acc = accs.tile([P, P], F32, name="acc", tag="acc")
+                    open_acc[2 * a + h] = acc
             for dd in range(DC):
                 d = (c % NDC) * DC + dd
-                nc.tensor.matmul(
-                    out=acc[:],
-                    lhsT=rt[:, dd, :],
-                    rhs=ident_f[:],
-                    is_transpose=True,
-                    start=(d == 0),
-                    stop=(d == EMB - 1),
+                for h in range(2):
+                    nc.tensor.matmul(
+                        out=open_acc[2 * a + h][:],
+                        lhsT=rt[:, h, dd, :],
+                        rhs=ident_f[:],
+                        is_transpose=True,
+                        start=(d == 0),
+                        stop=(d == EMB - 1),
+                    )
+
+        def extra_passes(count):
+            for w in range(count):
+                spare = idle.tile([P, CH], F32, name="spare", tag="spare")
+                nc.tensor.matmul_mx(
+                    out=spare[:],
+                    lhsT=we_codes[:].bitcast(FP8X4),
+                    lhsT_scale=we_scales[:],
+                    rhs=last_codes[:].bitcast(FP8X4),
+                    rhs_scale=last_scales[:],
+                    start=True,
+                    stop=True,
                 )
 
         roots = {}
@@ -255,16 +280,25 @@ def tile_hypernymvisual_acc_t_kernel(tc, vfs, p_lfs, n_lfs, W_hidden, b_hidden, 
                 if c < 0:
                     continue
                 square_and_add(c)
-                in_group = c % (TG * NDC)
-                if in_group % 4 == 0 and 8 <= in_group < 28:
-                    positives(c // (TG * NDC), (in_group - 8) // 4)
+                if c == 0:
+                    extra_passes(FIRST_WARM)
+                elif c % WARM_EVERY == 0:
+                    extra_passes(WARM)
+                in_group = c % (TG // 2 * NDC)
+                if in_group % 8 == 0 and 16 <= in_group < 56:
+                    positives(c // (TG // 2 * NDC), (in_group - 16) // 8)
                 if c >= NDC:
-                    if c % NDC == 0:
-                        finish_root(c // NDC - 1)
-                    if c % NDC == 2:
-                        finish_back(c // NDC - 1)
-                    if c % NDC == 5:
-                        finish_store(c // NDC - 1)
-            finish_root(NT - 1)
-            finish_back(NT - 1)
-            finish_store(NT - 1)
+                    for h in range(2):
+                        t = 2 * (c // NDC - 1) + h
+                        if c % NDC == 1:
+                            finish_root(t)
+                        if c % NDC == 5:
+                            finish_back(t)
+                        if c % NDC == 12:
+                            finish_store(t)
+            for h in range(2):
+                finish_root(NT - 2 + h)
+            for h in range(2):
+                finish_back(NT - 2 + h)
+            for h in range(2):
+                finish_store(NT - 2 + h)

@@ -27,8 +27,8 @@ NCHUNK = (NT // 2) * NDC
 VSQ = 70
 LEAD = 4
 FIRST_WARM = 6
-WARM_EVERY = 64
-WARM = 3
+WARM_EVERY = 2
+WARM = 1
 TG = 8
 
 FLOPS = 2 * B * VF * HID + 2 * B * HID * EMB + 4 * B * (NNEG + 1) * EMB

@@ -21,17 +21,36 @@ EMB = 128
 NNEG = 128
 CH = 512
 NCH = B // CH
-DC = 4
-NDC = EMB // DC
-NCHUNK = (NT // 2) * NDC
-VSQ = 70
+WG = 1024
+NG = B // WG
+TG = WG // P
+BPU = WG // CH
+JS = 87
+NV = NNEG - JS
 LEAD = 4
-FIRST_WARM = 6
-WARM_EVERY = 2
-WARM = 1
-TG = 8
+LAG_V = 2
+NJUNK = 8
+DEFER = 8
 
 FLOPS = 2 * B * VF * HID + 2 * B * HID * EMB + 4 * B * (NNEG + 1) * EMB
+
+
+def bank_steps():
+    steps = []
+    n_s = (JS + 1) * BPU
+    n_v = NV * BPU
+    total = n_s + n_v
+    for g in range(NG):
+        done_s = 0
+        done_v = 0
+        for k in range(total):
+            if (done_v + 1) * total <= (k + 1) * n_v:
+                steps.append((g, "v", done_v // BPU, done_v % BPU))
+                done_v += 1
+            else:
+                steps.append((g, "s", done_s // BPU, done_s % BPU))
+                done_s += 1
+    return steps
 
 
 def tile_hypernymvisual_acc_t_kernel(tc, vfs, p_lfs, n_lfs, W_hidden, b_hidden, W_embed, b_embed, out):
@@ -42,19 +61,17 @@ def tile_hypernymvisual_acc_t_kernel(tc, vfs, p_lfs, n_lfs, W_hidden, b_hidden, 
         masks.make_identity(nc, ident_f[:])
         ident_b = keep.tile([P, P], BF16, name="ident_b")
         masks.make_identity(nc, ident_b[:])
-        emb = keep.tile([P, NT, EMB], F32, name="emb")
-        n_bc = keep.tile([P, EMB, NNEG], F32, name="n_bc")
-        res = keep.tile([P, NT, NNEG + 1], F32, name="res")
+        eT = keep.tile([P, B], F32, name="eT")
+        rp = keep.tile([P, B], F32, name="rp")
+        nT = keep.tile([P, NNEG], F32, name="nT")
         bias = keep.tile([P, 8], F32, name="bias")
-        we_codes = keep.tile([P, EMB], U32, name="we_codes", align_bytes=64)
-        we_scales = keep.tile([P, EMB], U8, name="we_scales", align_bytes=64)
-        last_codes = keep.tile([P, CH], U32, name="last_codes", align_bytes=64)
-        last_scales = keep.tile([P, CH], U8, name="last_scales", align_bytes=64)
         warm = keep.tile([P, 2], F32, name="warm")
         nc.vector.memset(warm[:], 1.0)
         nc.scalar.activation(out=warm[:, 1:2], in_=warm[:, 0:1], func=ACT.Sqrt)
 
-        with tc.tile_pool(name="front", bufs=1) as fr, tc.tile_pool(name="stage", bufs=2) as stg, tc.psum_pool(name="fps", bufs=1) as fps:
+        fr = ctx.enter_context(tc.tile_pool(name="front", bufs=1))
+        stg = ctx.enter_context(tc.tile_pool(name="stage", bufs=3))
+        with tc.psum_pool(name="fps", bufs=1) as fps:
             wh_sb = fr.tile([P, 4 * VF], BF16, name="wh_sb")
             nc.sync.dma_start(
                 out=wh_sb[:].rearrange("p (m k) -> p m k", m=4),
@@ -66,29 +83,23 @@ def tile_hypernymvisual_acc_t_kernel(tc, vfs, p_lfs, n_lfs, W_hidden, b_hidden, 
             nc.sync.dma_start(out=x_sb[:, 0:step], in_=x_view[:, 0:step])
             we_sb = fr.tile([P, HID], BF16, name="we_sb")
             nc.sync.dma_start(out=we_sb[:], in_=W_embed)
+            n_sb = fr.tile([P, EMB], BF16, name="n_sb")
+            nc.sync.dma_start(out=n_sb[:], in_=n_lfs)
             zb = fr.tile([P, P], BF16, name="zb")
             nc.vector.memset(zb[:], 0.0)
             nc.sync.dma_start(out=zb[0:4, :], in_=b_hidden.rearrange("(m p) -> m p", p=P))
-            b_bc = fr.tile([P, EMB], BF16, name="b_bc")
-            nc.sync.dma_start(out=b_bc[:], in_=b_embed.partition_broadcast(P))
-            nb16 = fr.tile([P, NNEG * EMB], BF16, name="nb16")
-            nc.sync.dma_start(out=nb16[:], in_=n_lfs.rearrange("j d -> (j d)").partition_broadcast(P))
+            nc.sync.dma_start(out=zb[4:5, :], in_=b_embed.rearrange("(o p) -> o p", o=1))
             for c in range(1, 4):
                 nc.sync.dma_start(out=x_sb[:, c * step:(c + 1) * step], in_=x_view[:, c * step:(c + 1) * step])
+            p_sb = fr.tile([P, NT * EMB], BF16, name="p_sb")
+            nc.sync.dma_start(out=p_sb[:], in_=p_lfs.rearrange("(p t) d -> p (t d)", t=NT))
 
-            nb_view = nb16[:].rearrange("p (j d) -> p d j", d=EMB)
-            for c in range(16):
-                nc.gpsimd.tensor_scalar(
-                    out=n_bc[:, 8 * c:8 * c + 8, :],
-                    in0=nb_view[:, 8 * c:8 * c + 8, :],
-                    scalar1=1.0,
-                    scalar2=0.0,
-                    op0=ALU.mult,
-                    op1=ALU.add,
-                )
-
+            x_codes = fr.tile([P, B], U32, name="x_codes", align_bytes=64)
+            x_scales = fr.tile([P, B], U8, name="x_scales", align_bytes=64)
             wh_codes = fr.tile([P, HID], U32, name="wh_codes", align_bytes=64)
             wh_scales = fr.tile([P, HID], U8, name="wh_scales", align_bytes=64)
+            we_codes = fr.tile([P, EMB], U32, name="we_codes", align_bytes=64)
+            we_scales = fr.tile([P, EMB], U8, name="we_scales", align_bytes=64)
 
             def words_to_codes(src_words, first, codes, scales):
                 g = stg.tile([P, 4 * CH], BF16, name="g", tag="g", align_bytes=64)
@@ -109,6 +120,9 @@ def tile_hypernymvisual_acc_t_kernel(tc, vfs, p_lfs, n_lfs, W_hidden, b_hidden, 
                 nc.vector.quantize_mx(out=codes.bitcast(FP8X4), scales=scales, in_=g[:])
 
             words_to_codes(wh_sb[:].bitcast(F32), 0, wh_codes[:], wh_scales[:])
+            xw = x_sb[:].bitcast(F32)
+            for n in range(NCH):
+                words_to_codes(xw, 4 * n, x_codes[:, n * CH:(n + 1) * CH], x_scales[:, n * CH:(n + 1) * CH])
 
             tb = fps.tile([P, CH], BF16, name="tb", tag="tp", bufs=3)
             for t in range(4):
@@ -118,14 +132,13 @@ def tile_hypernymvisual_acc_t_kernel(tc, vfs, p_lfs, n_lfs, W_hidden, b_hidden, 
             nc.vector.quantize_mx(out=we_codes[:].bitcast(FP8X4), scales=we_scales[:], in_=g_we[:].rearrange("p d t -> p (d t)"))
 
             tn = fps.tile([P, CH], BF16, name="tn", tag="tp", bufs=3)
-            nc.tensor.transpose(tn[:, 0:P], zb[:], ident_b[:])
-            nc.vector.tensor_copy(out=bias[:, 0:4], in_=tn[:, 0:4])
+            nc.tensor.transpose(tn[:, 0:P], n_sb[:], ident_b[:])
+            nc.tensor.transpose(tn[:, P:2 * P], zb[:], ident_b[:])
+            nc.vector.tensor_copy(out=nT[:], in_=tn[:, 0:P])
+            nc.vector.tensor_copy(out=bias[:, 0:5], in_=tn[:, P:P + 5])
 
-            xw = x_sb[:].bitcast(F32)
             for n in range(NCH):
-                x_codes = stg.tile([P, CH], U32, name="x_codes", tag="x_codes", align_bytes=64)
-                x_scales = stg.tile([P, CH], U8, name="x_scales", tag="x_scales", align_bytes=64)
-                words_to_codes(xw, 4 * n, x_codes[:], x_scales[:])
+                cols = slice(n * CH, (n + 1) * CH)
                 hb = stg.tile([P, 4, CH], BF16, name="hb", tag="hb")
                 for m in range(4):
                     ph = fps.tile([P, CH], F32, name="ph", tag="ph", bufs=4)
@@ -133,172 +146,148 @@ def tile_hypernymvisual_acc_t_kernel(tc, vfs, p_lfs, n_lfs, W_hidden, b_hidden, 
                         out=ph[:],
                         lhsT=wh_codes[:, m * P:(m + 1) * P].bitcast(FP8X4),
                         lhsT_scale=wh_scales[:, m * P:(m + 1) * P],
-                        rhs=x_codes[:].bitcast(FP8X4),
-                        rhs_scale=x_scales[:],
+                        rhs=x_codes[:, cols].bitcast(FP8X4),
+                        rhs_scale=x_scales[:, cols],
                         start=True,
                         stop=True,
                     )
-                    nc.scalar.activation(out=hb[:, m, :], in_=ph[:], func=ACT.Identity, bias=bias[:, m:m + 1])
+                    if m == 3 and n % 2 == 0:
+                        nc.vector.tensor_scalar(out=hb[:, m, :], in0=ph[:], scalar1=bias[:, m:m + 1], scalar2=None, op0=ALU.add)
+                    else:
+                        nc.scalar.activation(out=hb[:, m, :], in_=ph[:], func=ACT.Identity, bias=bias[:, m:m + 1])
                 g2 = stg.tile([P, CH, 4], BF16, name="g2", tag="g2", align_bytes=64)
                 nc.vector.tensor_copy(
                     out=g2[:].rearrange("p (c i) t -> p c t i", i=4),
                     in_=hb[:].rearrange("p t (c i) -> p c t i", i=4),
                 )
-                if n == NCH - 1:
-                    h_codes = last_codes
-                    h_scales = last_scales
-                else:
-                    h_codes = stg.tile([P, CH], U32, name="h_codes", tag="h_codes", align_bytes=64)
-                    h_scales = stg.tile([P, CH], U8, name="h_scales", tag="h_scales", align_bytes=64)
+                h_codes = stg.tile([P, CH], U32, name="h_codes", tag="h_codes", align_bytes=64)
+                h_scales = stg.tile([P, CH], U8, name="h_scales", tag="h_scales", align_bytes=64)
                 nc.vector.quantize_mx(out=h_codes[:].bitcast(FP8X4), scales=h_scales[:], in_=g2[:].rearrange("p c t -> p (c t)"))
-                pe = fps.tile([P, 4, EMB], F32, name="pe", tag="pe", bufs=1)
-                for s in range(4):
-                    nc.tensor.matmul_mx(
-                        out=pe[:, s, :],
-                        lhsT=h_codes[:, s * P:(s + 1) * P].bitcast(FP8X4),
-                        lhsT_scale=h_scales[:, s * P:(s + 1) * P],
-                        rhs=we_codes[:].bitcast(FP8X4),
-                        rhs_scale=we_scales[:],
-                        start=True,
-                        stop=True,
-                    )
-                nc.vector.tensor_tensor(
-                    out=emb[:, 4 * n:4 * n + 4, :],
-                    in0=pe[:],
-                    in1=b_bc[:].unsqueeze(1).to_broadcast([P, 4, EMB]),
-                    op=ALU.add,
-                )
-
-        rpool = ctx.enter_context(tc.tile_pool(name="rpool", bufs=12))
-        small = ctx.enter_context(tc.tile_pool(name="small", bufs=4))
-        accs = ctx.enter_context(tc.psum_pool(name="accs", bufs=4))
-        backs = ctx.enter_context(tc.psum_pool(name="backs", bufs=2))
-        idle = ctx.enter_context(tc.psum_pool(name="idle", bufs=2))
-        out_view = out.rearrange("(p t) c -> p (t c)", t=NT)
-        pos = ctx.enter_context(tc.tile_pool(name="pos", bufs=1))
-        p_sb = pos.tile([P, NT, EMB], BF16, name="p_sb")
-        nc.sync.dma_start(out=p_sb[:].rearrange("p t d -> p (t d)"), in_=p_lfs.rearrange("(p t) d -> p (t d)", t=NT))
-        xp = pos.tile([P, NT, EMB], F32, name="xp")
-        sum_p = pos.tile([P, NT], F32, name="sum_p")
-
-        def positives(g, stage):
-            ts = slice(g * TG, (g + 1) * TG)
-            if stage == 0:
-                nc.vector.tensor_tensor(out=xp[:, ts, :], in0=p_sb[:, ts, :], in1=emb[:, ts, :], op=ALU.subtract)
-                nc.vector.tensor_scalar_max(out=xp[:, ts, :], in0=xp[:, ts, :], scalar1=0.0)
-            elif stage == 1:
-                nc.scalar.activation(out=xp[:, ts, :], in_=xp[:, ts, :], func=ACT.Square)
-            elif stage == 2:
-                nc.vector.tensor_reduce(out=sum_p[:, ts], in_=xp[:, ts, :], axis=AX.X, op=ALU.add)
-            elif stage == 3:
-                nc.scalar.activation(out=sum_p[:, ts], in_=sum_p[:, ts], func=ACT.Sqrt)
-            else:
-                nc.vector.tensor_scalar(out=res[:, ts, 0], in0=sum_p[:, ts], scalar1=-1.0, scalar2=None, op0=ALU.mult)
-        diffs = {}
-        open_acc = {}
-
-        def write_diffs(c):
-            a = c // NDC
-            rt = rpool.tile([P, 2, DC, NNEG], F32, name="rt", tag="rt")
-            for h in range(2):
-                for dd in range(DC):
-                    d = (c % NDC) * DC + dd
-                    nc.vector.tensor_scalar(
-                        out=rt[:, h, dd, :],
-                        in0=n_bc[:, d, :],
-                        scalar1=emb[:, 2 * a + h, d:d + 1],
-                        scalar2=0.0,
-                        op0=ALU.subtract,
-                        op1=ALU.max,
-                    )
-            diffs[c] = rt
-
-        def square_and_add(c):
-            a = c // NDC
-            rt = diffs[c]
-            if ((c + 1) * VSQ) // NCHUNK > (c * VSQ) // NCHUNK:
-                nc.vector.tensor_tensor(out=rt[:], in0=rt[:], in1=rt[:], op=ALU.mult)
-            else:
-                nc.scalar.activation(out=rt[:], in_=rt[:], func=ACT.Square)
-            if c % NDC == 0:
-                for h in range(2):
-                    acc = accs.tile([P, P], F32, name="acc", tag="acc")
-                    open_acc[2 * a + h] = acc
-            for dd in range(DC):
-                d = (c % NDC) * DC + dd
-                for h in range(2):
-                    nc.tensor.matmul(
-                        out=open_acc[2 * a + h][:],
-                        lhsT=rt[:, h, dd, :],
-                        rhs=ident_f[:],
-                        is_transpose=True,
-                        start=(d == 0),
-                        stop=(d == EMB - 1),
-                    )
-
-        def extra_passes(count):
-            for w in range(count):
-                spare = idle.tile([P, CH], F32, name="spare", tag="spare")
+                pe = fps.tile([P, CH], F32, name="pe", tag="pe", bufs=1)
                 nc.tensor.matmul_mx(
-                    out=spare[:],
+                    out=pe[:],
                     lhsT=we_codes[:].bitcast(FP8X4),
                     lhsT_scale=we_scales[:],
-                    rhs=last_codes[:].bitcast(FP8X4),
-                    rhs_scale=last_scales[:],
+                    rhs=h_codes[:].bitcast(FP8X4),
+                    rhs_scale=h_scales[:],
                     start=True,
                     stop=True,
                 )
+                nc.scalar.activation(out=eT[:, cols], in_=pe[:], func=ACT.Identity, bias=bias[:, 4:5])
 
-        roots = {}
-        backed = {}
+            for n in range(NCH):
+                cols = slice(n * CH, (n + 1) * CH)
+                tq = fps.tile([P, CH], BF16, name="tq", tag="tp", bufs=3)
+                for s in range(4):
+                    t = 4 * n + s
+                    nc.tensor.transpose(tq[:, s * P:(s + 1) * P], p_sb[:, t * EMB:(t + 1) * EMB], ident_b[:])
+                nc.vector.tensor_tensor(out=rp[:, cols], in0=eT[:, cols], in1=tq[:], op=ALU.subtract)
+                nc.vector.tensor_scalar_min(out=rp[:, cols], in0=rp[:, cols], scalar1=0.0)
 
-        def finish_root(t):
-            root = small.tile([P, P], F32, name="root", tag="root")
-            nc.scalar.activation(out=root[:], in_=open_acc[t][:], func=ACT.Sqrt)
-            roots[t] = root
+        acc = ctx.enter_context(tc.tile_pool(name="acc", bufs=2))
+        rpool = ctx.enter_context(tc.tile_pool(name="rpool", bufs=6))
+        banks = ctx.enter_context(tc.psum_pool(name="banks", bufs=8))
+        junk = keep.tile([P, NJUNK, P], F32, name="junk")
+        out_view = out.rearrange("(p t) c -> p (t c)", t=NT)
+        steps = bank_steps()
+        n_steps = len(steps)
+        per_group = n_steps // NG
+        diffs = {}
+        filled = {}
+        sums = {}
+        late = {}
 
-        def finish_back(t):
-            back = backs.tile([P, P], F32, name="back", tag="back")
-            nc.tensor.transpose(back[:], roots[t][:], ident_f[:])
-            backed[t] = back
+        def write_diff(k):
+            g, kind, u, q = steps[k]
+            if q != 0:
+                return
+            if kind == "s" and u == JS:
+                diffs[(g, kind, u)] = rp[:, g * WG:(g + 1) * WG]
+                return
+            j = u if kind == "s" else JS + u
+            rt = rpool.tile([P, WG], F32, name="rt", tag="rt")
+            nc.vector.tensor_scalar(
+                out=rt[:],
+                in0=eT[:, g * WG:(g + 1) * WG],
+                scalar1=nT[:, j:j + 1],
+                scalar2=0.0,
+                op0=ALU.subtract,
+                op1=ALU.min,
+            )
+            diffs[(g, kind, u)] = rt[:]
 
-        def finish_store(t):
-            nc.vector.tensor_scalar(out=res[:, t, 1:NNEG + 1], in0=backed[t][:], scalar1=-1.0, scalar2=None, op0=ALU.mult)
-            if (t + 1) % TG == 0:
-                width = TG * (NNEG + 1)
-                g = t // TG
-                nc.sync.dma_start(
-                    out=out_view[:, g * width:(g + 1) * width],
-                    in_=res[:, g * TG:(g + 1) * TG, :].rearrange("p t c -> p (t c)"),
-                )
+        def transpose_bank(k):
+            g, kind, u, q = steps[k]
+            r = diffs[(g, kind, u)]
+            bank = banks.tile([P, CH], F32, name="bank", tag="bank")
+            for s in range(4):
+                nc.tensor.transpose(bank[:, s * P:(s + 1) * P], r[:, q * CH + s * P:q * CH + (s + 1) * P], ident_f[:])
+            filled[k] = bank
+
+        def consume(k):
+            g, kind, u, q = steps[k]
+            if g not in sums:
+                sum_s = acc.tile([P, TG, JS + 1], F32, name="sum_s", tag="sum_s")
+                stats = acc.tile([P, NV * TG, 6], F32, name="stats", tag="stats")
+                sums[g] = (sum_s, stats)
+            sum_s, stats = sums[g]
+            bank = filled[k]
+            for s in range(4):
+                t = 4 * q + s
+                if kind == "s":
+                    col = 0 if u == JS else u + 1
+                    nc.scalar.activation(out=junk[:, (4 * k + s) % NJUNK, :], in_=bank[:, s * P:(s + 1) * P], func=ACT.Square, accum_out=sum_s[:, t, col:col + 1])
+                else:
+                    nc.vector.bn_stats(out=stats[:, u * TG + t, :], in_=bank[:, s * P:(s + 1) * P])
+
+        def finish_sums(g):
+            sum_s, stats = sums[g]
+            st = stats[:].rearrange("p n (h s) -> p (n h) s", h=2)
+            msq = acc.tile([P, NV * TG * 2], F32, name="msq", tag="msq")
+            nc.vector.tensor_tensor(out=msq[:], in0=st[:, :, 1], in1=st[:, :, 1], op=ALU.mult)
+            nc.vector.scalar_tensor_tensor(out=msq[:], in0=msq[:], scalar=float(EMB // 2), in1=st[:, :, 2], op0=ALU.mult, op1=ALU.add)
+            sum_v = acc.tile([P, NV * TG], F32, name="sum_v", tag="sum_v")
+            nc.vector.tensor_reduce(out=sum_v[:], in_=msq[:].rearrange("p (n h) -> p n h", h=2), axis=AX.X, op=ALU.add)
+            late[g] = sum_v
+
+        def finish_roots(g):
+            sum_s, stats = sums[g]
+            sum_v = late[g]
+            root = acc.tile([P, TG, NNEG + 1], F32, name="root", tag="root")
+            nc.scalar.activation(out=root[:, :, 0:JS + 1], in_=sum_s[:], func=ACT.Sqrt)
+            nc.scalar.activation(out=root[:, :, JS + 1:NNEG + 1], in_=sum_v[:].rearrange("p (v t) -> p t v", t=TG), func=ACT.Sqrt)
+            late[g] = root
+
+        def finish_store(g):
+            root = late[g]
+            res = acc.tile([P, TG * (NNEG + 1)], F32, name="res", tag="res")
+            nc.vector.tensor_scalar(out=res[:], in0=root[:].rearrange("p t c -> p (t c)"), scalar1=-1.0, scalar2=None, op0=ALU.mult)
+            width = TG * (NNEG + 1)
+            nc.sync.dma_start(out=out_view[:, g * width:(g + 1) * width], in_=res[:])
 
         with tc.manual_schedule():
-            for k in range(NCHUNK + LEAD):
-                if k < NCHUNK:
-                    write_diffs(k)
-                c = k - LEAD
-                if c < 0:
+            pending_v = []
+            for k in range(n_steps + LEAD):
+                if k < n_steps:
+                    write_diff(k)
+                b = k - LEAD
+                if b < 0:
                     continue
-                square_and_add(c)
-                if c == 0:
-                    extra_passes(FIRST_WARM)
-                elif c % WARM_EVERY == 0:
-                    extra_passes(WARM)
-                in_group = c % (TG // 2 * NDC)
-                if in_group % 8 == 0 and 16 <= in_group < 56:
-                    positives(c // (TG // 2 * NDC), (in_group - 16) // 8)
-                if c >= NDC:
-                    for h in range(2):
-                        t = 2 * (c // NDC - 1) + h
-                        if c % NDC == 1:
-                            finish_root(t)
-                        if c % NDC == 5:
-                            finish_back(t)
-                        if c % NDC == 12:
-                            finish_store(t)
-            for h in range(2):
-                finish_root(NT - 2 + h)
-            for h in range(2):
-                finish_back(NT - 2 + h)
-            for h in range(2):
-                finish_store(NT - 2 + h)
+                transpose_bank(b)
+                if steps[b][1] == "s":
+                    consume(b)
+                else:
+                    pending_v.append(b)
+                last_of_group = (b + 1) % per_group == 0
+                while pending_v and (pending_v[0] <= b - LAG_V or last_of_group):
+                    consume(pending_v[0])
+                    pending_v = pending_v[1:]
+                g_now = steps[b][0]
+                if last_of_group:
+                    finish_sums(g_now)
+                if g_now > 0 and b % per_group == DEFER:
+                    finish_roots(g_now - 1)
+                if g_now > 0 and b % per_group == 2 * DEFER:
+                    finish_store(g_now - 1)
+            finish_roots(NG - 1)
+            finish_store(NG - 1)

@@ -10,7 +10,6 @@ U8 = mybir.dt.uint8
 FP8X4 = mybir.dt.float8_e4m3fn_x4
 ALU = mybir.AluOpType
 ACT = mybir.ActivationFunctionType
-AX = mybir.AxisListType
 
 P = 128
 B = 4096
@@ -25,7 +24,7 @@ WG = 1024
 NG = B // WG
 TG = WG // P
 BPU = WG // CH
-JS = 87
+JS = 84
 NV = NNEG - JS
 LEAD = 4
 LAG_V = 2
@@ -228,26 +227,26 @@ def tile_hypernymvisual_acc_t_kernel(tc, vfs, p_lfs, n_lfs, W_hidden, b_hidden, 
             g, kind, u, q = steps[k]
             if g not in sums:
                 sum_s = acc.tile([P, TG, JS + 1], F32, name="sum_s", tag="sum_s")
-                stats = acc.tile([P, NV * TG, 6], F32, name="stats", tag="stats")
+                stats = acc.tile([P, NV * TG // 2, 6], F32, name="stats", tag="stats")
                 sums[g] = (sum_s, stats)
             sum_s, stats = sums[g]
             bank = filled[k]
-            for s in range(4):
-                t = 4 * q + s
-                if kind == "s":
-                    col = 0 if u == JS else u + 1
-                    nc.scalar.activation(out=junk[:, (4 * k + s) % NJUNK, :], in_=bank[:, s * P:(s + 1) * P], func=ACT.Square, accum_out=sum_s[:, t, col:col + 1])
-                else:
-                    nc.vector.bn_stats(out=stats[:, u * TG + t, :], in_=bank[:, s * P:(s + 1) * P])
+            if kind == "s":
+                col = 0 if u == JS else u + 1
+                for s in range(4):
+                    nc.scalar.activation(out=junk[:, (4 * k + s) % NJUNK, :], in_=bank[:, s * P:(s + 1) * P], func=ACT.Square, accum_out=sum_s[:, 4 * q + s, col:col + 1])
+            else:
+                for b in range(2):
+                    pair = bank[:, 2 * b * P:2 * (b + 1) * P].rearrange("p (h d) -> p d h", h=2)
+                    nc.vector.bn_stats(out=stats[:, (u * TG + 4 * q) // 2 + b, :], in_=pair)
 
         def finish_sums(g):
             sum_s, stats = sums[g]
             st = stats[:].rearrange("p n (h s) -> p (n h) s", h=2)
-            msq = acc.tile([P, NV * TG * 2], F32, name="msq", tag="msq")
+            msq = acc.tile([P, NV * TG], F32, name="msq", tag="msq")
             nc.vector.tensor_tensor(out=msq[:], in0=st[:, :, 1], in1=st[:, :, 1], op=ALU.mult)
-            nc.vector.scalar_tensor_tensor(out=msq[:], in0=msq[:], scalar=float(EMB // 2), in1=st[:, :, 2], op0=ALU.mult, op1=ALU.add)
             sum_v = acc.tile([P, NV * TG], F32, name="sum_v", tag="sum_v")
-            nc.vector.tensor_reduce(out=sum_v[:], in_=msq[:].rearrange("p (n h) -> p n h", h=2), axis=AX.X, op=ALU.add)
+            nc.vector.scalar_tensor_tensor(out=sum_v[:], in0=msq[:], scalar=float(EMB), in1=st[:, :, 2], op0=ALU.mult, op1=ALU.add)
             late[g] = sum_v
 
         def finish_roots(g):

@@ -10,6 +10,7 @@ U8 = mybir.dt.uint8
 FP8X4 = mybir.dt.float8_e4m3fn_x4
 ALU = mybir.AluOpType
 ACT = mybir.ActivationFunctionType
+AX = mybir.AxisListType
 
 P = 128
 B = 4096
@@ -20,57 +21,54 @@ EMB = 128
 NNEG = 128
 CH = 512
 NCH = B // CH
-WG = 1024
-NG = B // WG
-TG = WG // P
-BPU = WG // CH
-JS = 84
-NV = NNEG - JS
-LEAD = 4
-LAG_V = 2
-NJUNK = 8
-DEFER = 8
+TC = CH // P
+DL = 8
+H = EMB // DL
+JL = P // DL
+JH = NNEG // JL
+SET = 4
+HP = 2
+STEPS = NCH * JH * (H // HP)
+NSQ_V = 110
+LEAD = 6
+SQ = 2
+RBUFS = 10
+LAG_R = 3
 
 FLOPS = 2 * B * VF * HID + 2 * B * HID * EMB + 4 * B * (NNEG + 1) * EMB
 
 
-def bank_steps():
-    steps = []
-    n_s = (JS + 1) * BPU
-    n_v = NV * BPU
-    total = n_s + n_v
-    for g in range(NG):
-        done_s = 0
-        done_v = 0
-        for k in range(total):
-            if (done_v + 1) * total <= (k + 1) * n_v:
-                steps.append((g, "v", done_v // BPU, done_v % BPU))
-                done_v += 1
-            else:
-                steps.append((g, "s", done_s // BPU, done_s % BPU))
-                done_s += 1
-    return steps
-
-
 def tile_hypernymvisual_acc_t_kernel(tc, vfs, p_lfs, n_lfs, W_hidden, b_hidden, W_embed, b_embed, out):
     nc = tc.nc
+    scratch = out.rearrange("a b -> (a b)")[0:EMB * B].rearrange("(d c) -> d c", c=B)
     with ExitStack() as ctx:
         keep = ctx.enter_context(tc.tile_pool(name="keep", bufs=1))
         ident_f = keep.tile([P, P], F32, name="ident_f")
         masks.make_identity(nc, ident_f[:])
         ident_b = keep.tile([P, P], BF16, name="ident_b")
         masks.make_identity(nc, ident_b[:])
-        eT = keep.tile([P, B], F32, name="eT")
-        rp = keep.tile([P, B], F32, name="rp")
-        nT = keep.tile([P, NNEG], F32, name="nT")
+        n_raw = keep.tile([P, JH, H], BF16, name="n_raw")
+        n_tab = keep.tile([P, JH, H], F32, name="n_tab")
+        sums = keep.tile([P, NT, NNEG + 1], F32, name="sums")
         bias = keep.tile([P, 8], F32, name="bias")
         warm = keep.tile([P, 2], F32, name="warm")
         nc.vector.memset(warm[:], 1.0)
         nc.scalar.activation(out=warm[:, 1:2], in_=warm[:, 0:1], func=ACT.Sqrt)
+        junk = keep.tile([P, 4, P], F32, name="junk")
+        epool = ctx.enter_context(tc.tile_pool(name="epool", bufs=2))
+        e_rep = {}
 
-        fr = ctx.enter_context(tc.tile_pool(name="front", bufs=1))
-        stg = ctx.enter_context(tc.tile_pool(name="stage", bufs=3))
-        with tc.psum_pool(name="fps", bufs=1) as fps:
+        def load_e(c):
+            e = epool.tile([P, H, CH], F32, name="e", tag="e")
+            for dl in range(DL):
+                rows = scratch[dl * H:(dl + 1) * H, c * CH:(c + 1) * CH]
+                nc.sync.dma_start(out=e[dl:P:DL, :, :], in_=rows.partition_broadcast(JL))
+            e_rep[c] = e
+
+        with ExitStack() as front:
+            fr = front.enter_context(tc.tile_pool(name="front", bufs=1))
+            stg = front.enter_context(tc.tile_pool(name="stage", bufs=3))
+            fps = front.enter_context(tc.psum_pool(name="fps", bufs=1))
             wh_sb = fr.tile([P, 4 * VF], BF16, name="wh_sb")
             nc.sync.dma_start(
                 out=wh_sb[:].rearrange("p (m k) -> p m k", m=4),
@@ -82,8 +80,6 @@ def tile_hypernymvisual_acc_t_kernel(tc, vfs, p_lfs, n_lfs, W_hidden, b_hidden, 
             nc.sync.dma_start(out=x_sb[:, 0:step], in_=x_view[:, 0:step])
             we_sb = fr.tile([P, HID], BF16, name="we_sb")
             nc.sync.dma_start(out=we_sb[:], in_=W_embed)
-            n_sb = fr.tile([P, EMB], BF16, name="n_sb")
-            nc.sync.dma_start(out=n_sb[:], in_=n_lfs)
             zb = fr.tile([P, P], BF16, name="zb")
             nc.vector.memset(zb[:], 0.0)
             nc.sync.dma_start(out=zb[0:4, :], in_=b_hidden.rearrange("(m p) -> m p", p=P))
@@ -92,7 +88,11 @@ def tile_hypernymvisual_acc_t_kernel(tc, vfs, p_lfs, n_lfs, W_hidden, b_hidden, 
                 nc.sync.dma_start(out=x_sb[:, c * step:(c + 1) * step], in_=x_view[:, c * step:(c + 1) * step])
             p_sb = fr.tile([P, NT * EMB], BF16, name="p_sb")
             nc.sync.dma_start(out=p_sb[:], in_=p_lfs.rearrange("(p t) d -> p (t d)", t=NT))
+            n_view = n_lfs.rearrange("(jh jl) (dl h) -> dl jl jh h", jl=JL, dl=DL)
+            for dl in range(DL):
+                nc.sync.dma_start(out=n_raw[dl:P:DL, :, :], in_=n_view[dl])
 
+            eT = fr.tile([P, B], F32, name="eT")
             x_codes = fr.tile([P, B], U32, name="x_codes", align_bytes=64)
             x_scales = fr.tile([P, B], U8, name="x_scales", align_bytes=64)
             wh_codes = fr.tile([P, HID], U32, name="wh_codes", align_bytes=64)
@@ -131,10 +131,9 @@ def tile_hypernymvisual_acc_t_kernel(tc, vfs, p_lfs, n_lfs, W_hidden, b_hidden, 
             nc.vector.quantize_mx(out=we_codes[:].bitcast(FP8X4), scales=we_scales[:], in_=g_we[:].rearrange("p d t -> p (d t)"))
 
             tn = fps.tile([P, CH], BF16, name="tn", tag="tp", bufs=3)
-            nc.tensor.transpose(tn[:, 0:P], n_sb[:], ident_b[:])
-            nc.tensor.transpose(tn[:, P:2 * P], zb[:], ident_b[:])
-            nc.vector.tensor_copy(out=nT[:], in_=tn[:, 0:P])
-            nc.vector.tensor_copy(out=bias[:, 0:5], in_=tn[:, P:P + 5])
+            nc.tensor.transpose(tn[:, 0:P], zb[:], ident_b[:])
+            nc.vector.tensor_copy(out=bias[:, 0:5], in_=tn[:, 0:5])
+            nc.vector.tensor_copy(out=n_tab[:], in_=n_raw[:])
 
             for n in range(NCH):
                 cols = slice(n * CH, (n + 1) * CH)
@@ -173,120 +172,126 @@ def tile_hypernymvisual_acc_t_kernel(tc, vfs, p_lfs, n_lfs, W_hidden, b_hidden, 
                     stop=True,
                 )
                 nc.scalar.activation(out=eT[:, cols], in_=pe[:], func=ACT.Identity, bias=bias[:, 4:5])
+                nc.sync.dma_start(out=scratch[:, cols], in_=eT[:, cols])
+                if n < 2:
+                    load_e(n)
 
             for n in range(NCH):
                 cols = slice(n * CH, (n + 1) * CH)
                 tq = fps.tile([P, CH], BF16, name="tq", tag="tp", bufs=3)
-                for s in range(4):
-                    t = 4 * n + s
+                for s in range(TC):
+                    t = TC * n + s
                     nc.tensor.transpose(tq[:, s * P:(s + 1) * P], p_sb[:, t * EMB:(t + 1) * EMB], ident_b[:])
-                nc.vector.tensor_tensor(out=rp[:, cols], in0=eT[:, cols], in1=tq[:], op=ALU.subtract)
-                nc.vector.tensor_scalar_min(out=rp[:, cols], in0=rp[:, cols], scalar1=0.0)
+                rp = stg.tile([P, CH], F32, name="rp", tag="rp")
+                nc.vector.tensor_tensor(out=rp[:], in0=eT[:, cols], in1=tq[:], op=ALU.subtract)
+                nc.vector.tensor_scalar_min(out=rp[:], in0=rp[:], scalar1=0.0)
+                tr = fps.tile([P, CH], F32, name="tr", tag="tp", bufs=3)
+                for s in range(TC):
+                    nc.tensor.transpose(tr[:, s * P:(s + 1) * P], rp[:, s * P:(s + 1) * P], ident_f[:])
+                for s in range(TC):
+                    nc.scalar.activation(out=junk[:, s, :], in_=tr[:, s * P:(s + 1) * P], func=ACT.Square, accum_out=sums[:, TC * n + s, 0:1])
 
-        acc = ctx.enter_context(tc.tile_pool(name="acc", bufs=2))
-        rpool = ctx.enter_context(tc.tile_pool(name="rpool", bufs=6))
+        rpool = ctx.enter_context(tc.tile_pool(name="rpool", bufs=RBUFS))
+        fin = ctx.enter_context(tc.tile_pool(name="fin", bufs=2))
         banks = ctx.enter_context(tc.psum_pool(name="banks", bufs=8))
-        junk = keep.tile([P, NJUNK, P], F32, name="junk")
-        out_view = out.rearrange("(p t) c -> p (t c)", t=NT)
-        steps = bank_steps()
-        n_steps = len(steps)
-        per_group = n_steps // NG
-        diffs = {}
-        filled = {}
-        sums = {}
-        late = {}
+        out_view = out.rearrange("(p t) c -> p t c", t=NT)
+        per_jh = H // HP
+        per_chunk = JH * per_jh
+        tiles = {}
+        acc = {}
+        roots = {}
 
-        def write_diff(k):
-            g, kind, u, q = steps[k]
-            if q != 0:
-                return
-            if kind == "s" and u == JS:
-                diffs[(g, kind, u)] = rp[:, g * WG:(g + 1) * WG]
-                return
-            j = u if kind == "s" else JS + u
-            rt = rpool.tile([P, WG], F32, name="rt", tag="rt")
-            nc.vector.tensor_scalar(
-                out=rt[:],
-                in0=eT[:, g * WG:(g + 1) * WG],
-                scalar1=nT[:, j:j + 1],
-                scalar2=0.0,
-                op0=ALU.subtract,
-                op1=ALU.min,
-            )
-            diffs[(g, kind, u)] = rt[:]
+        def where(k):
+            return k // per_chunk, (k // per_jh) % JH, k % per_jh
 
-        def transpose_bank(k):
-            g, kind, u, q = steps[k]
-            r = diffs[(g, kind, u)]
-            bank = banks.tile([P, CH], F32, name="bank", tag="bank")
-            for s in range(4):
-                nc.tensor.transpose(bank[:, s * P:(s + 1) * P], r[:, q * CH + s * P:q * CH + (s + 1) * P], ident_f[:])
-            filled[k] = bank
+        def differences(k):
+            c, jh, hp = where(k)
+            r = rpool.tile([P, HP, CH], F32, name="r", tag="r")
+            for i in range(HP):
+                h = hp * HP + i
+                nc.vector.tensor_scalar(
+                    out=r[:, i, :],
+                    in0=e_rep[c][:, h, :],
+                    scalar1=n_tab[:, jh, h:h + 1],
+                    scalar2=0.0,
+                    op0=ALU.subtract,
+                    op1=ALU.min,
+                )
+            tiles[k] = r
 
-        def consume(k):
-            g, kind, u, q = steps[k]
-            if g not in sums:
-                sum_s = acc.tile([P, TG, JS + 1], F32, name="sum_s", tag="sum_s")
-                stats = acc.tile([P, NV * TG // 2, 6], F32, name="stats", tag="stats")
-                sums[g] = (sum_s, stats)
-            sum_s, stats = sums[g]
-            bank = filled[k]
-            if kind == "s":
-                col = 0 if u == JS else u + 1
-                for s in range(4):
-                    nc.scalar.activation(out=junk[:, (4 * k + s) % NJUNK, :], in_=bank[:, s * P:(s + 1) * P], func=ACT.Square, accum_out=sum_s[:, 4 * q + s, col:col + 1])
+        def square(k):
+            r = tiles[k]
+            if (k + 1) * NSQ_V // STEPS > k * NSQ_V // STEPS:
+                nc.vector.tensor_tensor(out=r[:], in0=r[:], in1=r[:], op=ALU.mult)
             else:
-                for b in range(2):
-                    pair = bank[:, 2 * b * P:2 * (b + 1) * P].rearrange("p (h d) -> p d h", h=2)
-                    nc.vector.bn_stats(out=stats[:, (u * TG + 4 * q) // 2 + b, :], in_=pair)
+                nc.scalar.activation(out=r[:], in_=r[:], func=ACT.Square)
 
-        def finish_sums(g):
-            sum_s, stats = sums[g]
-            st = stats[:].rearrange("p n (h s) -> p (n h) s", h=2)
-            msq = acc.tile([P, NV * TG], F32, name="msq", tag="msq")
-            nc.vector.tensor_tensor(out=msq[:], in0=st[:, :, 1], in1=st[:, :, 1], op=ALU.mult)
-            sum_v = acc.tile([P, NV * TG], F32, name="sum_v", tag="sum_v")
-            nc.vector.scalar_tensor_tensor(out=sum_v[:], in0=msq[:], scalar=float(EMB), in1=st[:, :, 2], op0=ALU.mult, op1=ALU.add)
-            late[g] = sum_v
+        def add_up(k):
+            c, jh, hp = where(k)
+            r = tiles[k]
+            if jh % SET == 0 and hp == 0:
+                acc[(c, jh // SET)] = []
+                for t in range(TC):
+                    bank = banks.tile([P, CH], F32, name="bank", tag="bank")
+                    acc[(c, jh // SET)].append(bank)
+            place = jh % SET
+            for i in range(HP):
+                h = hp * HP + i
+                for t in range(TC):
+                    nc.tensor.matmul(
+                        out=acc[(c, jh // SET)][t][:, place * P:(place + 1) * P],
+                        lhsT=r[:, i, t * P:(t + 1) * P],
+                        rhs=ident_f[:],
+                        is_transpose=True,
+                        start=(h == 0),
+                        stop=(h == H - 1),
+                    )
 
-        def finish_roots(g):
-            sum_s, stats = sums[g]
-            sum_v = late[g]
-            root = acc.tile([P, TG, NNEG + 1], F32, name="root", tag="root")
-            nc.scalar.activation(out=root[:, :, 0:JS + 1], in_=sum_s[:], func=ACT.Sqrt)
-            nc.scalar.activation(out=root[:, :, JS + 1:NNEG + 1], in_=sum_v[:].rearrange("p (v t) -> p t v", t=TG), func=ACT.Sqrt)
-            late[g] = root
+        def sum_dl(c, s):
+            for t in range(TC):
+                first = 1 + s * SET * JL
+                nc.vector.tensor_reduce(
+                    out=sums[:, c * TC + t, first:first + SET * JL],
+                    in_=acc[(c, s)][t][:].rearrange("p (g d) -> p g d", d=DL),
+                    axis=AX.X,
+                    op=ALU.add,
+                )
 
-        def finish_store(g):
-            root = late[g]
-            res = acc.tile([P, TG * (NNEG + 1)], F32, name="res", tag="res")
-            nc.vector.tensor_scalar(out=res[:], in0=root[:].rearrange("p t c -> p (t c)"), scalar1=-1.0, scalar2=None, op0=ALU.mult)
-            width = TG * (NNEG + 1)
-            nc.sync.dma_start(out=out_view[:, g * width:(g + 1) * width], in_=res[:])
+        def finish(c):
+            root = fin.tile([P, TC, NNEG + 1], F32, name="root", tag="root", bufs=NCH)
+            nc.scalar.activation(out=root[:], in_=sums[:, c * TC:(c + 1) * TC, :], func=ACT.Sqrt)
+            roots[c] = root
 
+        def negate(c):
+            nc.vector.tensor_scalar(out=roots[c][:], in0=roots[c][:], scalar1=-1.0, scalar2=None, op0=ALU.mult)
+
+        def store(c):
+            nc.sync.dma_start(out=out_view[:, c * TC:(c + 1) * TC, :], in_=roots[c][:])
+
+        per_set = SET * per_jh
         with tc.manual_schedule():
-            pending_v = []
-            for k in range(n_steps + LEAD):
-                if k < n_steps:
-                    write_diff(k)
+            for k in range(STEPS + LEAD + LAG_R + 9):
+                if k < STEPS:
+                    differences(k)
+                    if k % per_chunk == per_chunk - 1 and k // per_chunk + 2 < NCH:
+                        load_e(k // per_chunk + 2)
+                if 0 <= k - SQ < STEPS:
+                    square(k - SQ)
                 b = k - LEAD
-                if b < 0:
-                    continue
-                transpose_bank(b)
-                if steps[b][1] == "s":
-                    consume(b)
-                else:
-                    pending_v.append(b)
-                last_of_group = (b + 1) % per_group == 0
-                while pending_v and (pending_v[0] <= b - LAG_V or last_of_group):
-                    consume(pending_v[0])
-                    pending_v = pending_v[1:]
-                g_now = steps[b][0]
-                if last_of_group:
-                    finish_sums(g_now)
-                if g_now > 0 and b % per_group == DEFER:
-                    finish_roots(g_now - 1)
-                if g_now > 0 and b % per_group == 2 * DEFER:
-                    finish_store(g_now - 1)
-            finish_roots(NG - 1)
-            finish_store(NG - 1)
+                if 0 <= b < STEPS:
+                    add_up(b)
+                b = k - LEAD - LAG_R
+                if b >= 0 and b % per_set == per_set - 1 and b < STEPS:
+                    sum_dl(b // per_chunk, (b // per_set) % (JH // SET))
+                for lag, what in ((3, finish), (6, negate)):
+                    e = b - lag
+                    if e >= 0 and e % per_chunk == per_chunk - 1 and e < STEPS:
+                        what(e // per_chunk)
+                e = b - 8
+                if e >= 0 and e % per_chunk == per_chunk - 1 and e < STEPS:
+                    c = e // per_chunk
+                    if c == NCH - 3:
+                        for i in range(c + 1):
+                            store(i)
+                    elif c > NCH - 3:
+                        store(c)

@@ -28,8 +28,9 @@ JL = P // DL
 JH = NNEG // JL
 SET = 4
 HP = 2
+H_LOAD = 12
 STEPS = NCH * JH * (H // HP)
-NSQ_V = 110
+NSQ_V = 112
 LEAD = 6
 SQ = 2
 RBUFS = 10
@@ -55,15 +56,37 @@ def tile_hypernymvisual_acc_t_kernel(tc, vfs, p_lfs, n_lfs, W_hidden, b_hidden, 
         nc.vector.memset(warm[:], 1.0)
         nc.scalar.activation(out=warm[:, 1:2], in_=warm[:, 0:1], func=ACT.Sqrt)
         junk = keep.tile([P, 4, P], F32, name="junk")
+        h_codes = keep.tile([P, B], U32, name="h_codes", align_bytes=64)
+        h_scales = keep.tile([P, B], U8, name="h_scales", align_bytes=64)
+        rep_codes = keep.tile([P, H * P], U32, name="rep_codes", align_bytes=64)
+        rep_scales = keep.tile([P, H * P], U8, name="rep_scales", align_bytes=64)
+        b_raw = keep.tile([P, H], BF16, name="b_raw")
+        b_rep = keep.tile([P, H], F32, name="b_rep")
         epool = ctx.enter_context(tc.tile_pool(name="epool", bufs=2))
         e_rep = {}
 
         def load_e(c):
             e = epool.tile([P, H, CH], F32, name="e", tag="e")
             for dl in range(DL):
-                rows = scratch[dl * H:(dl + 1) * H, c * CH:(c + 1) * CH]
-                nc.sync.dma_start(out=e[dl:P:DL, :, :], in_=rows.partition_broadcast(JL))
+                rows = scratch[dl * H:dl * H + H_LOAD, c * CH:(c + 1) * CH]
+                nc.sync.dma_start(out=e[dl:P:DL, 0:H_LOAD, :], in_=rows.partition_broadcast(JL))
             e_rep[c] = e
+
+        def make_e(c, h, bank, engine):
+            cols = slice(c * CH, (c + 1) * CH)
+            nc.tensor.matmul_mx(
+                out=bank[:],
+                lhsT=rep_codes[:, h * P:(h + 1) * P].bitcast(FP8X4),
+                lhsT_scale=rep_scales[:, h * P:(h + 1) * P],
+                rhs=h_codes[:, cols].bitcast(FP8X4),
+                rhs_scale=h_scales[:, cols],
+                start=True,
+                stop=True,
+            )
+            if engine == "s":
+                nc.scalar.activation(out=e_rep[c][:, h, :], in_=bank[:], func=ACT.Identity, bias=b_rep[:, h:h + 1])
+            else:
+                nc.vector.tensor_scalar(out=e_rep[c][:, h, :], in0=bank[:], scalar1=b_rep[:, h:h + 1], scalar2=None, op0=ALU.add)
 
         with ExitStack() as front:
             fr = front.enter_context(tc.tile_pool(name="front", bufs=1))
@@ -91,10 +114,8 @@ def tile_hypernymvisual_acc_t_kernel(tc, vfs, p_lfs, n_lfs, W_hidden, b_hidden, 
             n_view = n_lfs.rearrange("(jh jl) (dl h) -> dl jl jh h", jl=JL, dl=DL)
             for dl in range(DL):
                 nc.sync.dma_start(out=n_raw[dl:P:DL, :, :], in_=n_view[dl])
+                nc.sync.dma_start(out=b_raw[dl:P:DL, :], in_=b_embed[dl * H:(dl + 1) * H].partition_broadcast(JL))
 
-            eT = fr.tile([P, B], F32, name="eT")
-            x_codes = fr.tile([P, B], U32, name="x_codes", align_bytes=64)
-            x_scales = fr.tile([P, B], U8, name="x_scales", align_bytes=64)
             wh_codes = fr.tile([P, HID], U32, name="wh_codes", align_bytes=64)
             wh_scales = fr.tile([P, HID], U8, name="wh_scales", align_bytes=64)
             we_codes = fr.tile([P, EMB], U32, name="we_codes", align_bytes=64)
@@ -120,8 +141,16 @@ def tile_hypernymvisual_acc_t_kernel(tc, vfs, p_lfs, n_lfs, W_hidden, b_hidden, 
 
             words_to_codes(wh_sb[:].bitcast(F32), 0, wh_codes[:], wh_scales[:])
             xw = x_sb[:].bitcast(F32)
-            for n in range(NCH):
-                words_to_codes(xw, 4 * n, x_codes[:, n * CH:(n + 1) * CH], x_scales[:, n * CH:(n + 1) * CH])
+            x_q = {}
+
+            def quantise_x(n):
+                x_codes = stg.tile([P, CH], U32, name="x_codes", tag="x_codes", align_bytes=64)
+                x_scales = stg.tile([P, CH], U8, name="x_scales", tag="x_scales", align_bytes=64)
+                words_to_codes(xw, 4 * n, x_codes[:], x_scales[:])
+                x_q[n] = (x_codes, x_scales)
+
+            quantise_x(0)
+            quantise_x(1)
 
             tb = fps.tile([P, CH], BF16, name="tb", tag="tp", bufs=3)
             for t in range(4):
@@ -129,14 +158,28 @@ def tile_hypernymvisual_acc_t_kernel(tc, vfs, p_lfs, n_lfs, W_hidden, b_hidden, 
             g_we = fr.tile([P, EMB, 4], BF16, name="g_we", align_bytes=64)
             nc.vector.tensor_copy(out=g_we[:], in_=tb[:].rearrange("p (t d) -> p d t", t=4))
             nc.vector.quantize_mx(out=we_codes[:].bitcast(FP8X4), scales=we_scales[:], in_=g_we[:].rearrange("p d t -> p (d t)"))
+            for h0 in range(0, H, 4):
+                g_rep = stg.tile([P, 4, JL, DL, 4], BF16, name="g_rep", tag="g_rep", align_bytes=64)
+                for h in range(h0, h0 + 4):
+                    src = g_we[:].rearrange("p (dl h) t -> p h dl t", h=H)[:, h]
+                    nc.vector.tensor_copy(out=g_rep[:, h - h0], in_=src.unsqueeze(1).to_broadcast([P, JL, DL, 4]))
+                nc.vector.quantize_mx(
+                    out=rep_codes[:, h0 * P:(h0 + 4) * P].bitcast(FP8X4),
+                    scales=rep_scales[:, h0 * P:(h0 + 4) * P],
+                    in_=g_rep[:].rearrange("p h jl dl t -> p (h jl dl t)"),
+                )
 
             tn = fps.tile([P, CH], BF16, name="tn", tag="tp", bufs=3)
             nc.tensor.transpose(tn[:, 0:P], zb[:], ident_b[:])
             nc.vector.tensor_copy(out=bias[:, 0:5], in_=tn[:, 0:5])
             nc.vector.tensor_copy(out=n_tab[:], in_=n_raw[:])
+            nc.vector.tensor_copy(out=b_rep[:], in_=b_raw[:])
 
             for n in range(NCH):
                 cols = slice(n * CH, (n + 1) * CH)
+                if n + 2 < NCH:
+                    quantise_x(n + 2)
+                x_codes, x_scales = x_q[n]
                 hb = stg.tile([P, 4, CH], BF16, name="hb", tag="hb")
                 for m in range(4):
                     ph = fps.tile([P, CH], F32, name="ph", tag="ph", bufs=4)
@@ -144,8 +187,8 @@ def tile_hypernymvisual_acc_t_kernel(tc, vfs, p_lfs, n_lfs, W_hidden, b_hidden, 
                         out=ph[:],
                         lhsT=wh_codes[:, m * P:(m + 1) * P].bitcast(FP8X4),
                         lhsT_scale=wh_scales[:, m * P:(m + 1) * P],
-                        rhs=x_codes[:, cols].bitcast(FP8X4),
-                        rhs_scale=x_scales[:, cols],
+                        rhs=x_codes[:].bitcast(FP8X4),
+                        rhs_scale=x_scales[:],
                         start=True,
                         stop=True,
                     )
@@ -158,32 +201,30 @@ def tile_hypernymvisual_acc_t_kernel(tc, vfs, p_lfs, n_lfs, W_hidden, b_hidden, 
                     out=g2[:].rearrange("p (c i) t -> p c t i", i=4),
                     in_=hb[:].rearrange("p t (c i) -> p c t i", i=4),
                 )
-                h_codes = stg.tile([P, CH], U32, name="h_codes", tag="h_codes", align_bytes=64)
-                h_scales = stg.tile([P, CH], U8, name="h_scales", tag="h_scales", align_bytes=64)
-                nc.vector.quantize_mx(out=h_codes[:].bitcast(FP8X4), scales=h_scales[:], in_=g2[:].rearrange("p c t -> p (c t)"))
+                nc.vector.quantize_mx(out=h_codes[:, cols].bitcast(FP8X4), scales=h_scales[:, cols], in_=g2[:].rearrange("p c t -> p (c t)"))
                 pe = fps.tile([P, CH], F32, name="pe", tag="pe", bufs=1)
                 nc.tensor.matmul_mx(
                     out=pe[:],
                     lhsT=we_codes[:].bitcast(FP8X4),
                     lhsT_scale=we_scales[:],
-                    rhs=h_codes[:].bitcast(FP8X4),
-                    rhs_scale=h_scales[:],
+                    rhs=h_codes[:, cols].bitcast(FP8X4),
+                    rhs_scale=h_scales[:, cols],
                     start=True,
                     stop=True,
                 )
-                nc.scalar.activation(out=eT[:, cols], in_=pe[:], func=ACT.Identity, bias=bias[:, 4:5])
-                nc.sync.dma_start(out=scratch[:, cols], in_=eT[:, cols])
-                if n < 2:
+                eT = stg.tile([P, CH], F32, name="eT", tag="eT")
+                nc.scalar.activation(out=eT[:], in_=pe[:], func=ACT.Identity, bias=bias[:, 4:5])
+                if n > 0:
+                    nc.sync.dma_start(out=scratch[:, cols], in_=eT[:])
+                if n == 1:
                     load_e(n)
 
-            for n in range(NCH):
-                cols = slice(n * CH, (n + 1) * CH)
                 tq = fps.tile([P, CH], BF16, name="tq", tag="tp", bufs=3)
                 for s in range(TC):
                     t = TC * n + s
                     nc.tensor.transpose(tq[:, s * P:(s + 1) * P], p_sb[:, t * EMB:(t + 1) * EMB], ident_b[:])
                 rp = stg.tile([P, CH], F32, name="rp", tag="rp")
-                nc.vector.tensor_tensor(out=rp[:], in0=eT[:, cols], in1=tq[:], op=ALU.subtract)
+                nc.vector.tensor_tensor(out=rp[:], in0=eT[:], in1=tq[:], op=ALU.subtract)
                 nc.vector.tensor_scalar_min(out=rp[:], in0=rp[:], scalar1=0.0)
                 tr = fps.tile([P, CH], F32, name="tr", tag="tp", bufs=3)
                 for s in range(TC):
@@ -191,9 +232,14 @@ def tile_hypernymvisual_acc_t_kernel(tc, vfs, p_lfs, n_lfs, W_hidden, b_hidden, 
                 for s in range(TC):
                     nc.scalar.activation(out=junk[:, s, :], in_=tr[:, s * P:(s + 1) * P], func=ACT.Square, accum_out=sums[:, TC * n + s, 0:1])
 
+            e_rep[0] = epool.tile([P, H, CH], F32, name="e", tag="e")
+            for h in range(H):
+                bank = fps.tile([P, CH], F32, name="bank", tag="ph", bufs=4)
+                make_e(0, h, bank, "sv"[h % 2])
+
         rpool = ctx.enter_context(tc.tile_pool(name="rpool", bufs=RBUFS))
         fin = ctx.enter_context(tc.tile_pool(name="fin", bufs=2))
-        banks = ctx.enter_context(tc.psum_pool(name="banks", bufs=8))
+        banks = ctx.enter_context(tc.psum_pool(name="banks", bufs=1))
         out_view = out.rearrange("(p t) c -> p t c", t=NT)
         per_jh = H // HP
         per_chunk = JH * per_jh
@@ -232,7 +278,7 @@ def tile_hypernymvisual_acc_t_kernel(tc, vfs, p_lfs, n_lfs, W_hidden, b_hidden, 
             if jh % SET == 0 and hp == 0:
                 acc[(c, jh // SET)] = []
                 for t in range(TC):
-                    bank = banks.tile([P, CH], F32, name="bank", tag="bank")
+                    bank = banks.tile([P, CH], F32, name="bank", tag="bank", bufs=7)
                     acc[(c, jh // SET)].append(bank)
             place = jh % SET
             for i in range(HP):
@@ -275,6 +321,10 @@ def tile_hypernymvisual_acc_t_kernel(tc, vfs, p_lfs, n_lfs, W_hidden, b_hidden, 
                     differences(k)
                     if k % per_chunk == per_chunk - 1 and k // per_chunk + 2 < NCH:
                         load_e(k // per_chunk + 2)
+                    c_next, r_next = k // per_chunk + 1, k % per_chunk
+                    if c_next < NCH and r_next % 8 == 4 and r_next < 8 * (H - H_LOAD):
+                        bank_e = banks.tile([P, CH], F32, name="bank_e", tag="bank_e", bufs=1)
+                        make_e(c_next, H_LOAD + r_next // 8, bank_e, "s")
                 if 0 <= k - SQ < STEPS:
                     square(k - SQ)
                 b = k - LEAD

@@ -10,7 +10,6 @@ U8 = mybir.dt.uint8
 FP8X4 = mybir.dt.float8_e4m3fn_x4
 ALU = mybir.AluOpType
 ACT = mybir.ActivationFunctionType
-AX = mybir.AxisListType
 
 P = 128
 B = 4096
@@ -22,243 +21,229 @@ NNEG = 128
 CH = 512
 NCH = B // CH
 TC = CH // P
-DL = 8
-H = EMB // DL
-JL = P // DL
-JH = NNEG // JL
-SET = 4
-HP = 2
-H_LOAD = 12
-STEPS = NCH * JH * (H // HP)
-NSQ_V = 112
+WIDE = 1024
+GROUPS = (512, 512, 1024, 1024, 1024)
+NSQ_V = 119
 LEAD = 6
 SQ = 2
-RBUFS = 10
-LAG_R = 3
+RBUFS = 14
+LAG_R = 1
+FRONT0 = 1
+FRONT = 8
 
 FLOPS = 2 * B * VF * HID + 2 * B * HID * EMB + 4 * B * (NNEG + 1) * EMB
 
 
 def tile_hypernymvisual_acc_t_kernel(tc, vfs, p_lfs, n_lfs, W_hidden, b_hidden, W_embed, b_embed, out):
     nc = tc.nc
-    scratch = out.rearrange("a b -> (a b)")[0:EMB * B].rearrange("(d c) -> d c", c=B)
+    out_flat = out.rearrange("a b -> (a b)")
+    out_view = out.rearrange("(p t) c -> p t c", t=NT)
     with ExitStack() as ctx:
         keep = ctx.enter_context(tc.tile_pool(name="keep", bufs=1))
-        ident_f = keep.tile([P, P], F32, name="ident_f")
-        masks.make_identity(nc, ident_f[:])
+        stg = ctx.enter_context(tc.tile_pool(name="stage", bufs=2))
+        rpool = ctx.enter_context(tc.tile_pool(name="rpool", bufs=RBUFS))
+        banks = ctx.enter_context(tc.psum_pool(name="banks", bufs=1))
+
+        def bank(i, dtype=F32):
+            return banks.tile([P, CH], dtype, name="b%d" % i, tag="b%d" % i)
+
+        n_sb = keep.tile([P, EMB], BF16, name="n_sb")
+        nc.sync.dma_start(out=n_sb[:], in_=n_lfs)
+        wh_sb = keep.tile([P, 4 * VF], BF16, name="wh_sb")
+        nc.sync.dma_start(out=wh_sb[:].rearrange("p (m k) -> p m k", m=4), in_=W_hidden.rearrange("(m p) k -> p m k", p=P))
+        x_view = vfs.rearrange("(p t) k -> p (t k)", t=NT)
+        x_sb = {}
+
+        def load_x(n):
+            x = keep.tile([P, TC * VF], BF16, name="x%d" % n)
+            nc.sync.dma_start(out=x[:], in_=x_view[:, n * TC * VF:(n + 1) * TC * VF])
+            x_sb[n] = x
+
+        load_x(0)
+        we_sb = keep.tile([P, HID], BF16, name="we_sb")
+        nc.sync.dma_start(out=we_sb[:], in_=W_embed)
+        zb = keep.tile([P, P], BF16, name="zb")
+        nc.vector.memset(zb[:], 0.0)
+        nc.sync.dma_start(out=zb[0:4, :], in_=b_hidden.rearrange("(m p) -> m p", p=P))
+        nc.sync.dma_start(out=zb[4:5, :], in_=b_embed.rearrange("(o p) -> o p", o=1))
+        load_x(1)
+
+        ident = keep.tile([P, 2 * P], F32, name="ident")
+        masks.make_identity(nc, ident[:, P:2 * P])
+        nc.vector.tensor_copy(out=ident[:, 0:P], in_=ident[:, P:2 * P])
+        ident_f = ident[:, P:2 * P]
         ident_b = keep.tile([P, P], BF16, name="ident_b")
         masks.make_identity(nc, ident_b[:])
-        n_raw = keep.tile([P, JH, H], BF16, name="n_raw")
-        n_tab = keep.tile([P, JH, H], F32, name="n_tab")
+        n_two = keep.tile([P, 2, NNEG], F32, name="n_two")
+        n_tab = keep.tile([P, NNEG], F32, name="n_tab")
         sums = keep.tile([P, NT, NNEG + 1], F32, name="sums")
+        eT = keep.tile([P, B], F32, name="eT")
         bias = keep.tile([P, 8], F32, name="bias")
         warm = keep.tile([P, 2], F32, name="warm")
         nc.vector.memset(warm[:], 1.0)
         nc.scalar.activation(out=warm[:, 1:2], in_=warm[:, 0:1], func=ACT.Sqrt)
         junk = keep.tile([P, 4, P], F32, name="junk")
-        h_codes = keep.tile([P, B], U32, name="h_codes", align_bytes=64)
-        h_scales = keep.tile([P, B], U8, name="h_scales", align_bytes=64)
-        rep_codes = keep.tile([P, H * P], U32, name="rep_codes", align_bytes=64)
-        rep_scales = keep.tile([P, H * P], U8, name="rep_scales", align_bytes=64)
-        b_raw = keep.tile([P, H], BF16, name="b_raw")
-        b_rep = keep.tile([P, H], F32, name="b_rep")
-        epool = ctx.enter_context(tc.tile_pool(name="epool", bufs=2))
-        e_rep = {}
+        wh_codes = keep.tile([P, HID], U32, name="wh_codes", align_bytes=64)
+        wh_scales = keep.tile([P, HID], U8, name="wh_scales", align_bytes=64)
+        we_codes = keep.tile([P, EMB], U32, name="we_codes", align_bytes=64)
+        we_scales = keep.tile([P, EMB], U8, name="we_scales", align_bytes=64)
+        g_of = {}
+        x_q = {}
+        h_q = {}
+        g2_of = {}
+        held = {}
 
-        def load_e(c):
-            e = epool.tile([P, H, CH], F32, name="e", tag="e")
-            for dl in range(DL):
-                rows = scratch[dl * H:dl * H + H_LOAD, c * CH:(c + 1) * CH]
-                nc.sync.dma_start(out=e[dl:P:DL, 0:H_LOAD, :], in_=rows.partition_broadcast(JL))
-            e_rep[c] = e
+        def turn_words(words, key, half, b):
+            if half == 0:
+                g_of[key] = stg.tile([P, 4 * CH], BF16, name="g", tag="g", align_bytes=64)
+            tp = bank(b)
+            for tt in range(2):
+                for u in range(2):
+                    blk = (2 * half + tt) * 256 + 128 * u
+                    nc.tensor.transpose(tp[:, (2 * tt + u) * P:(2 * tt + u + 1) * P], words[:, blk:blk + P], ident_f)
+            held[(key, half)] = tp
 
-        def make_e(c, h, bank, engine):
-            cols = slice(c * CH, (c + 1) * CH)
-            nc.tensor.matmul_mx(
-                out=bank[:],
-                lhsT=rep_codes[:, h * P:(h + 1) * P].bitcast(FP8X4),
-                lhsT_scale=rep_scales[:, h * P:(h + 1) * P],
-                rhs=h_codes[:, cols].bitcast(FP8X4),
-                rhs_scale=h_scales[:, cols],
-                start=True,
-                stop=True,
-            )
-            if engine == "s":
-                nc.scalar.activation(out=e_rep[c][:, h, :], in_=bank[:], func=ACT.Identity, bias=b_rep[:, h:h + 1])
-            else:
-                nc.vector.tensor_scalar(out=e_rep[c][:, h, :], in0=bank[:], scalar1=b_rep[:, h:h + 1], scalar2=None, op0=ALU.add)
+        def copy_words(key, half):
+            dst = g_of[key][:].bitcast(F32)[:, half * CH:(half + 1) * CH].rearrange("q (tt c u) -> q tt c u", tt=2, u=2)
+            nc.scalar.copy(out=dst, in_=held[(key, half)][:].rearrange("q (tt u c) -> q tt c u", tt=2, u=2))
 
-        with ExitStack() as front:
-            fr = front.enter_context(tc.tile_pool(name="front", bufs=1))
-            stg = front.enter_context(tc.tile_pool(name="stage", bufs=3))
-            fps = front.enter_context(tc.psum_pool(name="fps", bufs=1))
-            wh_sb = fr.tile([P, 4 * VF], BF16, name="wh_sb")
-            nc.sync.dma_start(
-                out=wh_sb[:].rearrange("p (m k) -> p m k", m=4),
-                in_=W_hidden.rearrange("(m p) k -> p m k", p=P),
-            )
-            x_sb = fr.tile([P, NT * VF], BF16, name="x_sb")
-            x_view = vfs.rearrange("(p t) k -> p (t k)", t=NT)
-            step = NT * VF // 4
-            nc.sync.dma_start(out=x_sb[:, 0:step], in_=x_view[:, 0:step])
-            we_sb = fr.tile([P, HID], BF16, name="we_sb")
-            nc.sync.dma_start(out=we_sb[:], in_=W_embed)
-            zb = fr.tile([P, P], BF16, name="zb")
-            nc.vector.memset(zb[:], 0.0)
-            nc.sync.dma_start(out=zb[0:4, :], in_=b_hidden.rearrange("(m p) -> m p", p=P))
-            nc.sync.dma_start(out=zb[4:5, :], in_=b_embed.rearrange("(o p) -> o p", o=1))
-            for c in range(1, 4):
-                nc.sync.dma_start(out=x_sb[:, c * step:(c + 1) * step], in_=x_view[:, c * step:(c + 1) * step])
-            p_sb = fr.tile([P, NT * EMB], BF16, name="p_sb")
-            nc.sync.dma_start(out=p_sb[:], in_=p_lfs.rearrange("(p t) d -> p (t d)", t=NT))
-            n_view = n_lfs.rearrange("(jh jl) (dl h) -> dl jl jh h", jl=JL, dl=DL)
-            for dl in range(DL):
-                nc.sync.dma_start(out=n_raw[dl:P:DL, :, :], in_=n_view[dl])
-                nc.sync.dma_start(out=b_raw[dl:P:DL, :], in_=b_embed[dl * H:(dl + 1) * H].partition_broadcast(JL))
+        def quantise_x(n):
+            x_codes = stg.tile([P, CH], U32, name="x_codes", tag="x_codes", align_bytes=64)
+            x_scales = stg.tile([P, CH], U8, name="x_scales", tag="x_scales", align_bytes=64)
+            nc.vector.quantize_mx(out=x_codes[:].bitcast(FP8X4), scales=x_scales[:], in_=g_of[n][:])
+            x_q[n] = (x_codes, x_scales)
 
-            wh_codes = fr.tile([P, HID], U32, name="wh_codes", align_bytes=64)
-            wh_scales = fr.tile([P, HID], U8, name="wh_scales", align_bytes=64)
-            we_codes = fr.tile([P, EMB], U32, name="we_codes", align_bytes=64)
-            we_scales = fr.tile([P, EMB], U8, name="we_scales", align_bytes=64)
-
-            def words_to_codes(src_words, first, codes, scales):
-                g = stg.tile([P, 4 * CH], BF16, name="g", tag="g", align_bytes=64)
-                gw = g[:].bitcast(F32)
-                for half in range(2):
-                    tp = fps.tile([P, CH], F32, name="tp", tag="tp", bufs=3)
-                    for tt in range(2):
-                        for u in range(2):
-                            blk = (first + 2 * half + tt) * 256 + 128 * u
-                            nc.tensor.transpose(
-                                tp[:, (2 * tt + u) * P:(2 * tt + u + 1) * P],
-                                src_words[:, blk:blk + P],
-                                ident_f[:],
-                            )
-                    dst = gw[:, half * CH:(half + 1) * CH].rearrange("q (tt c u) -> q tt c u", tt=2, u=2)
-                    src = tp[:].rearrange("q (tt u c) -> q tt c u", tt=2, u=2)
-                    nc.scalar.copy(out=dst, in_=src)
-                nc.vector.quantize_mx(out=codes.bitcast(FP8X4), scales=scales, in_=g[:])
-
-            words_to_codes(wh_sb[:].bitcast(F32), 0, wh_codes[:], wh_scales[:])
-            xw = x_sb[:].bitcast(F32)
-            x_q = {}
-
-            def quantise_x(n):
-                x_codes = stg.tile([P, CH], U32, name="x_codes", tag="x_codes", align_bytes=64)
-                x_scales = stg.tile([P, CH], U8, name="x_scales", tag="x_scales", align_bytes=64)
-                words_to_codes(xw, 4 * n, x_codes[:], x_scales[:])
-                x_q[n] = (x_codes, x_scales)
-
-            quantise_x(0)
-            quantise_x(1)
-
-            tb = fps.tile([P, CH], BF16, name="tb", tag="tp", bufs=3)
+        def hidden_mm(n, q, b):
+            x_codes, x_scales = x_q[n]
+            ph = bank(b)
             for t in range(4):
-                nc.tensor.transpose(tb[:, t * P:(t + 1) * P], we_sb[:, t * P:(t + 1) * P], ident_b[:])
-            g_we = fr.tile([P, EMB, 4], BF16, name="g_we", align_bytes=64)
-            nc.vector.tensor_copy(out=g_we[:], in_=tb[:].rearrange("p (t d) -> p d t", t=4))
-            nc.vector.quantize_mx(out=we_codes[:].bitcast(FP8X4), scales=we_scales[:], in_=g_we[:].rearrange("p d t -> p (d t)"))
-            for h0 in range(0, H, 4):
-                g_rep = stg.tile([P, 4, JL, DL, 4], BF16, name="g_rep", tag="g_rep", align_bytes=64)
-                for h in range(h0, h0 + 4):
-                    src = g_we[:].rearrange("p (dl h) t -> p h dl t", h=H)[:, h]
-                    nc.vector.tensor_copy(out=g_rep[:, h - h0], in_=src.unsqueeze(1).to_broadcast([P, JL, DL, 4]))
-                nc.vector.quantize_mx(
-                    out=rep_codes[:, h0 * P:(h0 + 4) * P].bitcast(FP8X4),
-                    scales=rep_scales[:, h0 * P:(h0 + 4) * P],
-                    in_=g_rep[:].rearrange("p h jl dl t -> p (h jl dl t)"),
-                )
-
-            tn = fps.tile([P, CH], BF16, name="tn", tag="tp", bufs=3)
-            nc.tensor.transpose(tn[:, 0:P], zb[:], ident_b[:])
-            nc.vector.tensor_copy(out=bias[:, 0:5], in_=tn[:, 0:5])
-            nc.vector.tensor_copy(out=n_tab[:], in_=n_raw[:])
-            nc.vector.tensor_copy(out=b_rep[:], in_=b_raw[:])
-
-            for n in range(NCH):
-                cols = slice(n * CH, (n + 1) * CH)
-                if n + 2 < NCH:
-                    quantise_x(n + 2)
-                x_codes, x_scales = x_q[n]
-                hb = stg.tile([P, 4, CH], BF16, name="hb", tag="hb")
-                for m in range(4):
-                    ph = fps.tile([P, CH], F32, name="ph", tag="ph", bufs=4)
-                    nc.tensor.matmul_mx(
-                        out=ph[:],
-                        lhsT=wh_codes[:, m * P:(m + 1) * P].bitcast(FP8X4),
-                        lhsT_scale=wh_scales[:, m * P:(m + 1) * P],
-                        rhs=x_codes[:].bitcast(FP8X4),
-                        rhs_scale=x_scales[:],
-                        start=True,
-                        stop=True,
-                    )
-                    if m == 3 and n % 2 == 0:
-                        nc.vector.tensor_scalar(out=hb[:, m, :], in0=ph[:], scalar1=bias[:, m:m + 1], scalar2=None, op0=ALU.add)
-                    else:
-                        nc.scalar.activation(out=hb[:, m, :], in_=ph[:], func=ACT.Identity, bias=bias[:, m:m + 1])
-                g2 = stg.tile([P, CH, 4], BF16, name="g2", tag="g2", align_bytes=64)
-                nc.vector.tensor_copy(
-                    out=g2[:].rearrange("p (c i) t -> p c t i", i=4),
-                    in_=hb[:].rearrange("p t (c i) -> p c t i", i=4),
-                )
-                nc.vector.quantize_mx(out=h_codes[:, cols].bitcast(FP8X4), scales=h_scales[:, cols], in_=g2[:].rearrange("p c t -> p (c t)"))
-                pe = fps.tile([P, CH], F32, name="pe", tag="pe", bufs=1)
                 nc.tensor.matmul_mx(
-                    out=pe[:],
-                    lhsT=we_codes[:].bitcast(FP8X4),
-                    lhsT_scale=we_scales[:],
-                    rhs=h_codes[:, cols].bitcast(FP8X4),
-                    rhs_scale=h_scales[:, cols],
+                    out=ph[:, t * P:(t + 1) * P],
+                    lhsT=wh_codes[:, t * P:(t + 1) * P].bitcast(FP8X4),
+                    lhsT_scale=wh_scales[:, t * P:(t + 1) * P],
+                    rhs=x_codes[:, q * P:(q + 1) * P].bitcast(FP8X4),
+                    rhs_scale=x_scales[:, q * P:(q + 1) * P],
                     start=True,
                     stop=True,
                 )
-                eT = stg.tile([P, CH], F32, name="eT", tag="eT")
-                nc.scalar.activation(out=eT[:], in_=pe[:], func=ACT.Identity, bias=bias[:, 4:5])
-                if n > 0:
-                    nc.sync.dma_start(out=scratch[:, cols], in_=eT[:])
-                if n == 1:
-                    load_e(n)
+            held[("ph", n, q)] = ph
 
-                tq = fps.tile([P, CH], BF16, name="tq", tag="tp", bufs=3)
-                for s in range(TC):
-                    t = TC * n + s
-                    nc.tensor.transpose(tq[:, s * P:(s + 1) * P], p_sb[:, t * EMB:(t + 1) * EMB], ident_b[:])
-                rp = stg.tile([P, CH], F32, name="rp", tag="rp")
-                nc.vector.tensor_tensor(out=rp[:], in0=eT[:], in1=tq[:], op=ALU.subtract)
-                nc.vector.tensor_scalar_min(out=rp[:], in0=rp[:], scalar1=0.0)
-                tr = fps.tile([P, CH], F32, name="tr", tag="tp", bufs=3)
-                for s in range(TC):
-                    nc.tensor.transpose(tr[:, s * P:(s + 1) * P], rp[:, s * P:(s + 1) * P], ident_f[:])
-                for s in range(TC):
-                    nc.scalar.activation(out=junk[:, s, :], in_=tr[:, s * P:(s + 1) * P], func=ACT.Square, accum_out=sums[:, TC * n + s, 0:1])
+        def hidden_add(n, q):
+            if q == 0:
+                g2_of[n] = stg.tile([P, CH, 4], BF16, name="g2", tag="g2", align_bytes=64)
+            nc.vector.tensor_tensor(
+                out=g2_of[n][:, q * P:(q + 1) * P, :],
+                in0=held[("ph", n, q)][:].rearrange("p (t c) -> p c t", t=4),
+                in1=bias[:, 0:4].unsqueeze(1).to_broadcast([P, P, 4]),
+                op=ALU.add,
+            )
 
-            e_rep[0] = epool.tile([P, H, CH], F32, name="e", tag="e")
-            for h in range(H):
-                bank = fps.tile([P, CH], F32, name="bank", tag="ph", bufs=4)
-                make_e(0, h, bank, "sv"[h % 2])
+        def quantise_h(n):
+            h_codes = stg.tile([P, CH], U32, name="h_codes", tag="h_codes", align_bytes=64)
+            h_scales = stg.tile([P, CH], U8, name="h_scales", tag="h_scales", align_bytes=64)
+            nc.vector.quantize_mx(out=h_codes[:].bitcast(FP8X4), scales=h_scales[:], in_=g2_of[n][:].rearrange("p c t -> p (c t)"))
+            h_q[n] = (h_codes, h_scales)
 
-        rpool = ctx.enter_context(tc.tile_pool(name="rpool", bufs=RBUFS))
-        fin = ctx.enter_context(tc.tile_pool(name="fin", bufs=2))
-        banks = ctx.enter_context(tc.psum_pool(name="banks", bufs=1))
-        out_view = out.rearrange("(p t) c -> p t c", t=NT)
-        per_jh = H // HP
-        per_chunk = JH * per_jh
+        def e_mm(n, b):
+            h_codes, h_scales = h_q[n]
+            pe = bank(b)
+            nc.tensor.matmul_mx(
+                out=pe[:],
+                lhsT=we_codes[:].bitcast(FP8X4),
+                lhsT_scale=we_scales[:],
+                rhs=h_codes[:].bitcast(FP8X4),
+                rhs_scale=h_scales[:],
+                start=True,
+                stop=True,
+            )
+            held[("e", n)] = pe
+
+        def e_copy(n):
+            nc.scalar.activation(out=eT[:, n * CH:(n + 1) * CH], in_=held[("e", n)][:], func=ACT.Identity, bias=bias[:, 4:5])
+
+        def pos_turn(n, b):
+            tq = bank(b, BF16)
+            for s in range(TC):
+                t = TC * n + s
+                nc.tensor.transpose(tq[:, s * P:(s + 1) * P], p_sb[:, t * EMB:(t + 1) * EMB], ident_b[:])
+            held[("tq", n)] = tq
+
+        def pos_diff(n):
+            rp = stg.tile([P, CH], F32, name="rp", tag="rp")
+            nc.vector.tensor_tensor(out=rp[:], in0=eT[:, n * CH:(n + 1) * CH], in1=held[("tq", n)][:], op=ALU.subtract)
+            nc.vector.tensor_scalar_min(out=rp[:], in0=rp[:], scalar1=0.0)
+            held[("rp", n)] = rp
+
+        def pos_back(n, b):
+            tr = bank(b)
+            for s in range(TC):
+                nc.tensor.transpose(tr[:, s * P:(s + 1) * P], held[("rp", n)][:, s * P:(s + 1) * P], ident_f)
+            held[("tr", n)] = tr
+
+        def pos_sum(n):
+            for s in range(TC):
+                nc.scalar.activation(out=junk[:, s, :], in_=held[("tr", n)][:, s * P:(s + 1) * P], func=ACT.Square, accum_out=sums[:, TC * n + s, 0:1])
+
+        tn = bank(4, BF16)
+        nc.tensor.transpose(tn[:, 0:P], n_sb[:], ident_b[:])
+        for i in range(2):
+            nc.vector.tensor_copy(out=n_two[:, i, :], in_=tn[:, 0:P])
+        nc.sync.dma_start(out=out_flat[0:P * 2 * NNEG].rearrange("(d c) -> d c", c=2 * NNEG), in_=n_two[:].rearrange("p i j -> p (i j)"))
+        nc.sync.dma_start(out=n_tab[:], in_=out_flat[0:P * (2 * NNEG + 1)].rearrange("(d c) -> d c", c=2 * NNEG + 1)[:, 0:NNEG])
+        p_sb = keep.tile([P, NT * EMB], BF16, name="p_sb")
+        for n in range(2, NCH):
+            load_x(n)
+            if n == 2:
+                nc.sync.dma_start(out=p_sb[:], in_=p_lfs.rearrange("(p t) d -> p (t d)", t=NT))
+
+        for half in range(2):
+            turn_words(wh_sb[:].bitcast(F32), "wh", half, half)
+            copy_words("wh", half)
+        nc.vector.quantize_mx(out=wh_codes[:].bitcast(FP8X4), scales=wh_scales[:], in_=g_of["wh"][:])
+        for half in range(2):
+            turn_words(x_sb[0][:].bitcast(F32), 0, half, 2 + half)
+            copy_words(0, half)
+        quantise_x(0)
+
+        tz = bank(4, BF16)
+        nc.tensor.transpose(tz[:, 0:P], zb[:], ident_b[:])
+        nc.vector.tensor_copy(out=bias[:, 0:5], in_=tz[:, 0:5])
+
+        tb = bank(5, BF16)
+        for t in range(4):
+            nc.tensor.transpose(tb[:, t * P:(t + 1) * P], we_sb[:, t * P:(t + 1) * P], ident_b[:])
+        g_we = keep.tile([P, EMB, 4], BF16, name="g_we", align_bytes=64)
+        nc.vector.tensor_copy(out=g_we[:], in_=tb[:].rearrange("p (t d) -> p d t", t=4))
+        nc.vector.quantize_mx(out=we_codes[:].bitcast(FP8X4), scales=we_scales[:], in_=g_we[:].rearrange("p d t -> p (d t)"))
+        for q in range(4):
+            hidden_mm(0, q, 6 + q % 2)
+            hidden_add(0, q)
+        quantise_h(0)
+        e_mm(0, 5)
+        e_copy(0)
+
+        steps = []
+        last_of = {}
+        col = 0
+        for g, width in enumerate(GROUPS):
+            many = WIDE // width
+            for s in range(0, NNEG, many):
+                steps.append((g, col, width, s, many))
+            last_of[len(steps) - 1] = g
+            col += width
+        n_steps = len(steps)
         tiles = {}
         acc = {}
-        roots = {}
-
-        def where(k):
-            return k // per_chunk, (k // per_jh) % JH, k % per_jh
+        bank_order = (0, 1, 2, 3, 4, 0, 1, 2, 3, 5, 6, 7, 4, 0, 1, 2, 3, 5, 6, 7, 4, 0, 1, 2, 3, 5, 6, 7, 4, 0, 1, 2)
 
         def differences(k):
-            c, jh, hp = where(k)
-            r = rpool.tile([P, HP, CH], F32, name="r", tag="r")
-            for i in range(HP):
-                h = hp * HP + i
+            g, col, width, s0, many = steps[k]
+            r = rpool.tile([P, WIDE], F32, name="r", tag="r")
+            for i in range(many):
                 nc.vector.tensor_scalar(
-                    out=r[:, i, :],
-                    in0=e_rep[c][:, h, :],
-                    scalar1=n_tab[:, jh, h:h + 1],
+                    out=r[:, i * width:(i + 1) * width],
+                    in0=eT[:, col:col + width],
+                    scalar1=n_tab[:, s0 + i:s0 + i + 1],
                     scalar2=0.0,
                     op0=ALU.subtract,
                     op1=ALU.min,
@@ -267,81 +252,87 @@ def tile_hypernymvisual_acc_t_kernel(tc, vfs, p_lfs, n_lfs, W_hidden, b_hidden, 
 
         def square(k):
             r = tiles[k]
-            if (k + 1) * NSQ_V // STEPS > k * NSQ_V // STEPS:
+            if (k + 1) * NSQ_V // n_steps > k * NSQ_V // n_steps:
                 nc.vector.tensor_tensor(out=r[:], in0=r[:], in1=r[:], op=ALU.mult)
             else:
                 nc.scalar.activation(out=r[:], in_=r[:], func=ACT.Square)
 
         def add_up(k):
-            c, jh, hp = where(k)
-            r = tiles[k]
-            if jh % SET == 0 and hp == 0:
-                acc[(c, jh // SET)] = []
-                for t in range(TC):
-                    bank = banks.tile([P, CH], F32, name="bank", tag="bank", bufs=7)
-                    acc[(c, jh // SET)].append(bank)
-            place = jh % SET
-            for i in range(HP):
-                h = hp * HP + i
-                for t in range(TC):
+            g, col, width, s0, many = steps[k]
+            if s0 == 0:
+                acc[g] = []
+            for i in range(many):
+                s = s0 + i
+                for t in range(width // P):
+                    if len(acc[g]) < width // P:
+                        acc[g].append(bank(bank_order[col // P + t]))
                     nc.tensor.matmul(
-                        out=acc[(c, jh // SET)][t][:, place * P:(place + 1) * P],
-                        lhsT=r[:, i, t * P:(t + 1) * P],
-                        rhs=ident_f[:],
+                        out=acc[g][t][:, 0:P],
+                        lhsT=tiles[k][:, i * width + t * P:i * width + (t + 1) * P],
+                        rhs=ident[:, P - s:2 * P - s],
                         is_transpose=True,
-                        start=(h == 0),
-                        stop=(h == H - 1),
+                        start=(s == 0),
+                        stop=(s == NNEG - 1),
                     )
 
-        def sum_dl(c, s):
-            for t in range(TC):
-                first = 1 + s * SET * JL
-                nc.vector.tensor_reduce(
-                    out=sums[:, c * TC + t, first:first + SET * JL],
-                    in_=acc[(c, s)][t][:].rearrange("p (g d) -> p g d", d=DL),
-                    axis=AX.X,
-                    op=ALU.add,
-                )
+        def group_tiles(g):
+            first = sum(GROUPS[:g]) // P
+            return first, first + GROUPS[g] // P
 
-        def finish(c):
-            root = fin.tile([P, TC, NNEG + 1], F32, name="root", tag="root", bufs=NCH)
-            nc.scalar.activation(out=root[:], in_=sums[:, c * TC:(c + 1) * TC, :], func=ACT.Sqrt)
-            roots[c] = root
+        def roots(g):
+            first, last = group_tiles(g)
+            for t in range(first, last):
+                nc.scalar.activation(out=sums[:, t, 1:NNEG + 1], in_=acc[g][t - first][:, 0:P], func=ACT.Sqrt)
 
-        def negate(c):
-            nc.vector.tensor_scalar(out=roots[c][:], in0=roots[c][:], scalar1=-1.0, scalar2=None, op0=ALU.mult)
+        def root_pos():
+            nc.scalar.activation(out=sums[:, :, 0], in_=sums[:, :, 0], func=ACT.Sqrt)
 
-        def store(c):
-            nc.sync.dma_start(out=out_view[:, c * TC:(c + 1) * TC, :], in_=roots[c][:])
+        def negate(g):
+            first, last = group_tiles(g)
+            nc.vector.tensor_scalar(out=sums[:, first:last, :], in0=sums[:, first:last, :], scalar1=-1.0, scalar2=None, op0=ALU.mult)
 
-        per_set = SET * per_jh
+        def store(g):
+            first, last = group_tiles(g)
+            nc.sync.dma_start(out=out_view[:, first:last, :], in_=sums[:, first:last, :])
+
+        extra = {}
+
+        def at(k, what, *args):
+            extra.setdefault(k, []).append((what, args))
+
+        for n in range(NCH):
+            o = FRONT0 + (n - 1) * FRONT
+            if n > 0:
+                for half in range(2):
+                    at(o + 2 * half, lambda n, half: turn_words(x_sb[n][:].bitcast(F32), n, half, 5), n, half)
+                    at(o + 2 * half + 1, copy_words, n, half)
+                at(o + 5, quantise_x, n)
+                for q in range(4):
+                    at(o + 6 + 2 * q, hidden_mm, n, q, 6)
+                    at(o + 7 + 2 * q, hidden_add, n, q)
+                at(o + 15, quantise_h, n)
+                at(o + 16, e_mm, n, 7)
+                at(o + 17, e_copy, n)
+            at(o + 20, pos_turn, n, 5)
+            at(o + 21, pos_diff, n)
+            at(o + 22, pos_back, n, 5)
+            at(o + 23, pos_sum, n)
+        at(FRONT0 + (NCH - 2) * FRONT + 25, root_pos)
+
         with tc.manual_schedule():
-            for k in range(STEPS + LEAD + LAG_R + 9):
-                if k < STEPS:
+            for k in range(n_steps + LEAD + LAG_R + 6):
+                if k < n_steps:
                     differences(k)
-                    if k % per_chunk == per_chunk - 1 and k // per_chunk + 2 < NCH:
-                        load_e(k // per_chunk + 2)
-                    c_next, r_next = k // per_chunk + 1, k % per_chunk
-                    if c_next < NCH and r_next % 8 == 4 and r_next < 8 * (H - H_LOAD):
-                        bank_e = banks.tile([P, CH], F32, name="bank_e", tag="bank_e", bufs=1)
-                        make_e(c_next, H_LOAD + r_next // 8, bank_e, "s")
-                if 0 <= k - SQ < STEPS:
+                for what, args in extra.get(k, []):
+                    what(*args)
+                if 0 <= k - SQ < n_steps:
                     square(k - SQ)
                 b = k - LEAD
-                if 0 <= b < STEPS:
+                if 0 <= b < n_steps:
                     add_up(b)
-                b = k - LEAD - LAG_R
-                if b >= 0 and b % per_set == per_set - 1 and b < STEPS:
-                    sum_dl(b // per_chunk, (b // per_set) % (JH // SET))
-                for lag, what in ((3, finish), (6, negate)):
-                    e = b - lag
-                    if e >= 0 and e % per_chunk == per_chunk - 1 and e < STEPS:
-                        what(e // per_chunk)
-                e = b - 8
-                if e >= 0 and e % per_chunk == per_chunk - 1 and e < STEPS:
-                    c = e // per_chunk
-                    if c == NCH - 3:
-                        for i in range(c + 1):
-                            store(i)
-                    elif c > NCH - 3:
-                        store(c)
+                for lag, what in ((LAG_R, roots), (LAG_R + 2, negate), (LAG_R + 3, store)):
+                    if b - lag in last_of:
+                        if b - lag > 63 or what == roots:
+                            what(last_of[b - lag])
+                        else:
+                            at(k + 40, what, last_of[b - lag])

@@ -22,14 +22,16 @@ CH = 512
 NCH = B // CH
 TC = CH // P
 WIDE = 1024
-GROUPS = (512, 512, 1024, 1024, 1024)
-NSQ_V = 119
-LEAD = 6
-SQ = 2
-RBUFS = 14
+GROUPS = (512, 1024, 1024, 1024, 512)
+SHARE_FRONT = 0.17
+SHARE = 0.245
+LEAD = 8
+SQ = 4
+RBUFS = 16
 LAG_R = 1
-FRONT0 = 1
-FRONT = 8
+FRONT0 = -5
+FRONT = 6
+FRONT_END = FRONT0 + (NCH - 2) * FRONT + 19
 
 FLOPS = 2 * B * VF * HID + 2 * B * HID * EMB + 4 * B * (NNEG + 1) * EMB
 
@@ -95,7 +97,7 @@ def tile_hypernymvisual_acc_t_kernel(tc, vfs, p_lfs, n_lfs, W_hidden, b_hidden, 
 
         def turn_words(words, key, half, b):
             if half == 0:
-                g_of[key] = stg.tile([P, 4 * CH], BF16, name="g", tag="g", align_bytes=64)
+                g_of[key] = stg.tile([P, 4 * CH], BF16, name="g", tag="g", bufs=3, align_bytes=64)
             tp = bank(b)
             for tt in range(2):
                 for u in range(2):
@@ -103,9 +105,9 @@ def tile_hypernymvisual_acc_t_kernel(tc, vfs, p_lfs, n_lfs, W_hidden, b_hidden, 
                     nc.tensor.transpose(tp[:, (2 * tt + u) * P:(2 * tt + u + 1) * P], words[:, blk:blk + P], ident_f)
             held[(key, half)] = tp
 
-        def copy_words(key, half):
+        def copy_words(key, half, copy=nc.scalar.copy):
             dst = g_of[key][:].bitcast(F32)[:, half * CH:(half + 1) * CH].rearrange("q (tt c u) -> q tt c u", tt=2, u=2)
-            nc.scalar.copy(out=dst, in_=held[(key, half)][:].rearrange("q (tt u c) -> q tt c u", tt=2, u=2))
+            copy(out=dst, in_=held[(key, half)][:].rearrange("q (tt u c) -> q tt c u", tt=2, u=2))
 
         def quantise_x(n):
             x_codes = stg.tile([P, CH], U32, name="x_codes", tag="x_codes", align_bytes=64)
@@ -198,7 +200,7 @@ def tile_hypernymvisual_acc_t_kernel(tc, vfs, p_lfs, n_lfs, W_hidden, b_hidden, 
 
         for half in range(2):
             turn_words(wh_sb[:].bitcast(F32), "wh", half, half)
-            copy_words("wh", half)
+            copy_words("wh", half, nc.vector.tensor_copy)
         nc.vector.quantize_mx(out=wh_codes[:].bitcast(FP8X4), scales=wh_scales[:], in_=g_of["wh"][:])
         for half in range(2):
             turn_words(x_sb[0][:].bitcast(F32), 0, half, 2 + half)
@@ -221,6 +223,10 @@ def tile_hypernymvisual_acc_t_kernel(tc, vfs, p_lfs, n_lfs, W_hidden, b_hidden, 
         quantise_h(0)
         e_mm(0, 5)
         e_copy(0)
+        for half in range(2):
+            turn_words(x_sb[1][:].bitcast(F32), 1, half, half)
+            copy_words(1, half)
+        quantise_x(1)
 
         steps = []
         last_of = {}
@@ -234,7 +240,7 @@ def tile_hypernymvisual_acc_t_kernel(tc, vfs, p_lfs, n_lfs, W_hidden, b_hidden, 
         n_steps = len(steps)
         tiles = {}
         acc = {}
-        bank_order = (0, 1, 2, 3, 4, 0, 1, 2, 3, 5, 6, 7, 4, 0, 1, 2, 3, 5, 6, 7, 4, 0, 1, 2, 3, 5, 6, 7, 4, 0, 1, 2)
+        bank_order = (0, 1, 2, 3) + (4, 5, 6, 7, 0, 1, 2, 3) * 3 + (4, 5, 6, 7)
 
         def differences(k):
             g, col, width, s0, many = steps[k]
@@ -250,9 +256,12 @@ def tile_hypernymvisual_acc_t_kernel(tc, vfs, p_lfs, n_lfs, W_hidden, b_hidden, 
                 )
             tiles[k] = r
 
+        def vector_squares(k):
+            return int(SHARE_FRONT * min(k, FRONT_END) + SHARE * max(k - FRONT_END, 0))
+
         def square(k):
             r = tiles[k]
-            if (k + 1) * NSQ_V // n_steps > k * NSQ_V // n_steps:
+            if vector_squares(k + 1) > vector_squares(k):
                 nc.vector.tensor_tensor(out=r[:], in0=r[:], in1=r[:], op=ALU.mult)
             else:
                 nc.scalar.activation(out=r[:], in_=r[:], func=ACT.Square)
@@ -303,21 +312,22 @@ def tile_hypernymvisual_acc_t_kernel(tc, vfs, p_lfs, n_lfs, W_hidden, b_hidden, 
         for n in range(NCH):
             o = FRONT0 + (n - 1) * FRONT
             if n > 0:
-                for half in range(2):
+                for half in range(2 if n > 1 else 0):
                     at(o + 2 * half, lambda n, half: turn_words(x_sb[n][:].bitcast(F32), n, half, 5), n, half)
                     at(o + 2 * half + 1, copy_words, n, half)
-                at(o + 5, quantise_x, n)
+                if n > 1:
+                    at(o + 5, quantise_x, n)
                 for q in range(4):
-                    at(o + 6 + 2 * q, hidden_mm, n, q, 6)
-                    at(o + 7 + 2 * q, hidden_add, n, q)
-                at(o + 15, quantise_h, n)
-                at(o + 16, e_mm, n, 7)
-                at(o + 17, e_copy, n)
-            at(o + 20, pos_turn, n, 5)
-            at(o + 21, pos_diff, n)
-            at(o + 22, pos_back, n, 5)
-            at(o + 23, pos_sum, n)
-        at(FRONT0 + (NCH - 2) * FRONT + 25, root_pos)
+                    at(o + 6 + q, hidden_mm, n, q, 4 + 2 * (q % 2))
+                    at(o + 7 + q, hidden_add, n, q)
+                at(o + 12, quantise_h, n)
+                at(o + 13, e_mm, n, 7)
+                at(o + 14, e_copy, n)
+            at(max(o + 15, 5), pos_turn, n, 7)
+            at(max(o + 16, 6), pos_diff, n)
+            at(max(o + 17, 7), pos_back, n, 7)
+            at(max(o + 18, 8), pos_sum, n)
+        at(FRONT_END + 1, root_pos)
 
         with tc.manual_schedule():
             for k in range(n_steps + LEAD + LAG_R + 6):
@@ -332,7 +342,4 @@ def tile_hypernymvisual_acc_t_kernel(tc, vfs, p_lfs, n_lfs, W_hidden, b_hidden, 
                     add_up(b)
                 for lag, what in ((LAG_R, roots), (LAG_R + 2, negate), (LAG_R + 3, store)):
                     if b - lag in last_of:
-                        if b - lag > 63 or what == roots:
-                            what(last_of[b - lag])
-                        else:
-                            at(k + 40, what, last_of[b - lag])
+                        what(last_of[b - lag])

@@ -21,17 +21,14 @@ NNEG = 128
 CH = 512
 NCH = B // CH
 TC = CH // P
-WIDE = 1024
-GROUPS = (512, 1024, 1024, 1024, 512)
-SHARE_FRONT = 0.17
-SHARE = 0.245
-LEAD = 8
-SQ = 4
-RBUFS = 16
+GROUPS = ((512, 2, 1024, 0.19), (1536, 1, 768, 0.225), (2048, 1, 1024, 0.235))
+WIDE = 2048
+LEAD = 6
+SQ = 3
+RBUFS = 8
 LAG_R = 1
-FRONT0 = -5
-FRONT = 6
-FRONT_END = FRONT0 + (NCH - 2) * FRONT + 19
+FRONT = (-11, -5, 8, 26, 48, 76, 104, 132)
+FRONT_END = FRONT[-1] + 19
 
 FLOPS = 2 * B * VF * HID + 2 * B * HID * EMB + 4 * B * (NNEG + 1) * EMB
 
@@ -230,17 +227,20 @@ def tile_hypernymvisual_acc_t_kernel(tc, vfs, p_lfs, n_lfs, W_hidden, b_hidden, 
 
         steps = []
         last_of = {}
+        share = {}
         col = 0
-        for g, width in enumerate(GROUPS):
-            many = WIDE // width
+        due = 0.0
+        for g, (width, many, part, want) in enumerate(GROUPS):
             for s in range(0, NNEG, many):
+                due += want * many * width / part
+                share[len(steps)] = part if due >= 1.0 else 0
+                due -= 1.0 if due >= 1.0 else 0.0
                 steps.append((g, col, width, s, many))
             last_of[len(steps) - 1] = g
             col += width
         n_steps = len(steps)
         tiles = {}
         acc = {}
-        bank_order = (0, 1, 2, 3) + (4, 5, 6, 7, 0, 1, 2, 3) * 3 + (4, 5, 6, 7)
 
         def differences(k):
             g, col, width, s0, many = steps[k]
@@ -256,53 +256,57 @@ def tile_hypernymvisual_acc_t_kernel(tc, vfs, p_lfs, n_lfs, W_hidden, b_hidden, 
                 )
             tiles[k] = r
 
-        def vector_squares(k):
-            return int(SHARE_FRONT * min(k, FRONT_END) + SHARE * max(k - FRONT_END, 0))
-
         def square(k):
+            g, col, width, s0, many = steps[k]
             r = tiles[k]
-            if vector_squares(k + 1) > vector_squares(k):
-                nc.vector.tensor_tensor(out=r[:], in0=r[:], in1=r[:], op=ALU.mult)
-            else:
-                nc.scalar.activation(out=r[:], in_=r[:], func=ACT.Square)
+            cut = many * width - share[k]
+            if share[k]:
+                nc.vector.tensor_tensor(out=r[:, cut:many * width], in0=r[:, cut:many * width], in1=r[:, cut:many * width], op=ALU.mult)
+            if cut:
+                nc.scalar.activation(out=r[:, 0:cut], in_=r[:, 0:cut], func=ACT.Square)
 
         def add_up(k):
             g, col, width, s0, many = steps[k]
             if s0 == 0:
-                acc[g] = []
+                acc[g] = [bank(b) for b in range(col // CH, (col + width) // CH)]
             for i in range(many):
                 s = s0 + i
                 for t in range(width // P):
-                    if len(acc[g]) < width // P:
-                        acc[g].append(bank(bank_order[col // P + t]))
                     nc.tensor.matmul(
-                        out=acc[g][t][:, 0:P],
+                        out=acc[g][t // TC][:, t % TC * P:(t % TC + 1) * P],
                         lhsT=tiles[k][:, i * width + t * P:i * width + (t + 1) * P],
                         rhs=ident[:, P - s:2 * P - s],
                         is_transpose=True,
-                        start=(s == 0),
-                        stop=(s == NNEG - 1),
+                        start=(s == 0 and t % TC == 0),
+                        stop=(s == NNEG - 1 and t % TC == TC - 1),
                     )
 
-        def group_tiles(g):
-            first = sum(GROUPS[:g]) // P
-            return first, first + GROUPS[g] // P
+        def chunks_of(g):
+            first = sum(width for width, many, part, want in GROUPS[:g]) // CH
+            return first, first + GROUPS[g][0] // CH
 
         def roots(g):
-            first, last = group_tiles(g)
-            for t in range(first, last):
-                nc.scalar.activation(out=sums[:, t, 1:NNEG + 1], in_=acc[g][t - first][:, 0:P], func=ACT.Sqrt)
+            first, last = chunks_of(g)
+            for c in range(first, last):
+                nc.scalar.activation(
+                    out=sums[:, c * TC:(c + 1) * TC, 1:NNEG + 1],
+                    in_=acc[g][c - first][:].rearrange("p (t j) -> p t j", t=TC),
+                    func=ACT.Sqrt,
+                )
 
         def root_pos():
             nc.scalar.activation(out=sums[:, :, 0], in_=sums[:, :, 0], func=ACT.Sqrt)
 
         def negate(g):
-            first, last = group_tiles(g)
-            nc.vector.tensor_scalar(out=sums[:, first:last, :], in0=sums[:, first:last, :], scalar1=-1.0, scalar2=None, op0=ALU.mult)
+            first, last = chunks_of(g)
+            for c in range(first, last):
+                part = sums[:, c * TC:(c + 1) * TC, :]
+                nc.vector.tensor_scalar(out=part, in0=part, scalar1=-1.0, scalar2=None, op0=ALU.mult)
 
         def store(g):
-            first, last = group_tiles(g)
-            nc.sync.dma_start(out=out_view[:, first:last, :], in_=sums[:, first:last, :])
+            first, last = chunks_of(g)
+            for c in range(first, last):
+                nc.sync.dma_start(out=out_view[:, c * TC:(c + 1) * TC, :], in_=sums[:, c * TC:(c + 1) * TC, :])
 
         extra = {}
 
@@ -310,7 +314,7 @@ def tile_hypernymvisual_acc_t_kernel(tc, vfs, p_lfs, n_lfs, W_hidden, b_hidden, 
             extra.setdefault(k, []).append((what, args))
 
         for n in range(NCH):
-            o = FRONT0 + (n - 1) * FRONT
+            o = FRONT[n]
             if n > 0:
                 for half in range(2 if n > 1 else 0):
                     at(o + 2 * half, lambda n, half: turn_words(x_sb[n][:].bitcast(F32), n, half, 5), n, half)
@@ -342,4 +346,7 @@ def tile_hypernymvisual_acc_t_kernel(tc, vfs, p_lfs, n_lfs, W_hidden, b_hidden, 
                     add_up(b)
                 for lag, what in ((LAG_R, roots), (LAG_R + 2, negate), (LAG_R + 3, store)):
                     if b - lag in last_of:
-                        what(last_of[b - lag])
+                        if what == roots or b - lag > FRONT_END:
+                            what(last_of[b - lag])
+                        else:
+                            at(max(k + 1, FRONT_END + 3), what, last_of[b - lag])

@@ -21,14 +21,15 @@ NNEG = 128
 CH = 512
 NCH = B // CH
 TC = CH // P
-GROUPS = ((512, 2, 1024, 0.19), (1536, 1, 768, 0.225), (2048, 1, 1024, 0.235))
+GROUPS = ((512, 2, 1, 0.19), (1536, 1, 2, 0.233), (2048, 1, 2, 0.243))
 WIDE = 2048
 LEAD = 6
 SQ = 3
 RBUFS = 8
 LAG_R = 1
-FRONT = (-11, -5, 8, 26, 48, 76, 104, 132)
-FRONT_END = FRONT[-1] + 19
+EARLY = 4
+FRONT = (-13, -5, 9, 23, 44, 72, 100, 128)
+FRONT_END = FRONT[-1] + 23
 
 FLOPS = 2 * B * VF * HID + 2 * B * HID * EMB + 4 * B * (NNEG + 1) * EMB
 
@@ -46,10 +47,7 @@ def tile_hypernymvisual_acc_t_kernel(tc, vfs, p_lfs, n_lfs, W_hidden, b_hidden, 
         def bank(i, dtype=F32):
             return banks.tile([P, CH], dtype, name="b%d" % i, tag="b%d" % i)
 
-        n_sb = keep.tile([P, EMB], BF16, name="n_sb")
-        nc.sync.dma_start(out=n_sb[:], in_=n_lfs)
         wh_sb = keep.tile([P, 4 * VF], BF16, name="wh_sb")
-        nc.sync.dma_start(out=wh_sb[:].rearrange("p (m k) -> p m k", m=4), in_=W_hidden.rearrange("(m p) k -> p m k", p=P))
         x_view = vfs.rearrange("(p t) k -> p (t k)", t=NT)
         x_sb = {}
 
@@ -58,7 +56,16 @@ def tile_hypernymvisual_acc_t_kernel(tc, vfs, p_lfs, n_lfs, W_hidden, b_hidden, 
             nc.sync.dma_start(out=x[:], in_=x_view[:, n * TC * VF:(n + 1) * TC * VF])
             x_sb[n] = x
 
-        load_x(0)
+        x_sb[0] = keep.tile([P, TC * VF], BF16, name="x0")
+        for half in range(2):
+            rows = slice(half * 2 * VF, (half + 1) * 2 * VF)
+            nc.sync.dma_start(
+                out=wh_sb[:, rows].rearrange("p (m k) -> p m k", m=2),
+                in_=W_hidden[half * 2 * P:(half + 1) * 2 * P, :].rearrange("(m p) k -> p m k", p=P),
+            )
+            nc.sync.dma_start(out=x_sb[0][:, rows], in_=x_view[:, rows])
+        n_sb = keep.tile([P, EMB], BF16, name="n_sb")
+        nc.sync.dma_start(out=n_sb[:], in_=n_lfs)
         we_sb = keep.tile([P, HID], BF16, name="we_sb")
         nc.sync.dma_start(out=we_sb[:], in_=W_embed)
         zb = keep.tile([P, P], BF16, name="zb")
@@ -81,7 +88,8 @@ def tile_hypernymvisual_acc_t_kernel(tc, vfs, p_lfs, n_lfs, W_hidden, b_hidden, 
         warm = keep.tile([P, 2], F32, name="warm")
         nc.vector.memset(warm[:], 1.0)
         nc.scalar.activation(out=warm[:, 1:2], in_=warm[:, 0:1], func=ACT.Sqrt)
-        junk = keep.tile([P, 4, P], F32, name="junk")
+        ones = keep.tile([P, 2], F32, name="ones")
+        nc.vector.memset(ones[:], 1.0)
         wh_codes = keep.tile([P, HID], U32, name="wh_codes", align_bytes=64)
         wh_scales = keep.tile([P, HID], U8, name="wh_scales", align_bytes=64)
         we_codes = keep.tile([P, EMB], U32, name="we_codes", align_bytes=64)
@@ -94,7 +102,7 @@ def tile_hypernymvisual_acc_t_kernel(tc, vfs, p_lfs, n_lfs, W_hidden, b_hidden, 
 
         def turn_words(words, key, half, b):
             if half == 0:
-                g_of[key] = stg.tile([P, 4 * CH], BF16, name="g", tag="g", bufs=3, align_bytes=64)
+                g_of[key] = stg.tile([P, 4 * CH], BF16, name="g", tag="g", bufs=5, align_bytes=64)
             tp = bank(b)
             for tt in range(2):
                 for u in range(2):
@@ -106,11 +114,15 @@ def tile_hypernymvisual_acc_t_kernel(tc, vfs, p_lfs, n_lfs, W_hidden, b_hidden, 
             dst = g_of[key][:].bitcast(F32)[:, half * CH:(half + 1) * CH].rearrange("q (tt c u) -> q tt c u", tt=2, u=2)
             copy(out=dst, in_=held[(key, half)][:].rearrange("q (tt u c) -> q tt c u", tt=2, u=2))
 
-        def quantise_x(n):
-            x_codes = stg.tile([P, CH], U32, name="x_codes", tag="x_codes", align_bytes=64)
-            x_scales = stg.tile([P, CH], U8, name="x_scales", tag="x_scales", align_bytes=64)
-            nc.vector.quantize_mx(out=x_codes[:].bitcast(FP8X4), scales=x_scales[:], in_=g_of[n][:])
-            x_q[n] = (x_codes, x_scales)
+        def quantise(src, codes, scales, cols):
+            nc.vector.quantize_mx(out=codes[:, cols].bitcast(FP8X4), scales=scales[:, cols], in_=src[:, 4 * cols.start:4 * cols.stop])
+
+        def quantise_x(n, cols=slice(0, CH)):
+            if cols.start == 0:
+                x_codes = stg.tile([P, CH], U32, name="x_codes", tag="x_codes", bufs=4, align_bytes=64)
+                x_scales = stg.tile([P, CH], U8, name="x_scales", tag="x_scales", bufs=4, align_bytes=64)
+                x_q[n] = (x_codes, x_scales)
+            quantise(g_of[n], x_q[n][0], x_q[n][1], cols)
 
         def hidden_mm(n, q, b):
             x_codes, x_scales = x_q[n]
@@ -137,28 +149,29 @@ def tile_hypernymvisual_acc_t_kernel(tc, vfs, p_lfs, n_lfs, W_hidden, b_hidden, 
                 op=ALU.add,
             )
 
-        def quantise_h(n):
-            h_codes = stg.tile([P, CH], U32, name="h_codes", tag="h_codes", align_bytes=64)
-            h_scales = stg.tile([P, CH], U8, name="h_scales", tag="h_scales", align_bytes=64)
-            nc.vector.quantize_mx(out=h_codes[:].bitcast(FP8X4), scales=h_scales[:], in_=g2_of[n][:].rearrange("p c t -> p (c t)"))
-            h_q[n] = (h_codes, h_scales)
+        def quantise_h(n, cols=slice(0, CH)):
+            if cols.start == 0:
+                h_codes = stg.tile([P, CH], U32, name="h_codes", tag="h_codes", align_bytes=64)
+                h_scales = stg.tile([P, CH], U8, name="h_scales", tag="h_scales", align_bytes=64)
+                h_q[n] = (h_codes, h_scales)
+            quantise(g2_of[n][:].rearrange("p c t -> p (c t)"), h_q[n][0], h_q[n][1], cols)
 
-        def e_mm(n, b):
+        def e_mm(n, b, cols=slice(0, CH)):
             h_codes, h_scales = h_q[n]
             pe = bank(b)
             nc.tensor.matmul_mx(
-                out=pe[:],
+                out=pe[:, cols],
                 lhsT=we_codes[:].bitcast(FP8X4),
                 lhsT_scale=we_scales[:],
-                rhs=h_codes[:].bitcast(FP8X4),
-                rhs_scale=h_scales[:],
+                rhs=h_codes[:, cols].bitcast(FP8X4),
+                rhs_scale=h_scales[:, cols],
                 start=True,
                 stop=True,
             )
             held[("e", n)] = pe
 
-        def e_copy(n):
-            nc.scalar.activation(out=eT[:, n * CH:(n + 1) * CH], in_=held[("e", n)][:], func=ACT.Identity, bias=bias[:, 4:5])
+        def e_copy(n, cols=slice(0, CH)):
+            nc.scalar.activation(out=eT[:, n * CH + cols.start:n * CH + cols.stop], in_=held[("e", n)][:, cols], func=ACT.Identity, bias=bias[:, 4:5])
 
         def pos_turn(n, b):
             tq = bank(b, BF16)
@@ -170,18 +183,20 @@ def tile_hypernymvisual_acc_t_kernel(tc, vfs, p_lfs, n_lfs, W_hidden, b_hidden, 
         def pos_diff(n):
             rp = stg.tile([P, CH], F32, name="rp", tag="rp")
             nc.vector.tensor_tensor(out=rp[:], in0=eT[:, n * CH:(n + 1) * CH], in1=held[("tq", n)][:], op=ALU.subtract)
-            nc.vector.tensor_scalar_min(out=rp[:], in0=rp[:], scalar1=0.0)
             held[("rp", n)] = rp
 
-        def pos_back(n, b):
+        def pos_square(n):
+            rp = held[("rp", n)]
+            nc.vector.scalar_tensor_tensor(out=rp[:], in0=rp[:], scalar=0.0, in1=rp[:], op0=ALU.min, op1=ALU.mult)
+
+        def pos_sum(n, b):
             tr = bank(b)
             for s in range(TC):
-                nc.tensor.transpose(tr[:, s * P:(s + 1) * P], held[("rp", n)][:, s * P:(s + 1) * P], ident_f)
+                nc.tensor.matmul(out=tr[:, s:s + 1], lhsT=held[("rp", n)][:, s * P:(s + 1) * P], rhs=ones[:, 0:1], start=True, stop=True)
             held[("tr", n)] = tr
 
-        def pos_sum(n):
-            for s in range(TC):
-                nc.scalar.activation(out=junk[:, s, :], in_=held[("tr", n)][:, s * P:(s + 1) * P], func=ACT.Square, accum_out=sums[:, TC * n + s, 0:1])
+        def pos_root(n):
+            nc.scalar.activation(out=sums[:, TC * n:TC * (n + 1), 0], in_=held[("tr", n)][:, 0:TC], func=ACT.Sqrt)
 
         tn = bank(4, BF16)
         nc.tensor.transpose(tn[:, 0:P], n_sb[:], ident_b[:])
@@ -195,14 +210,15 @@ def tile_hypernymvisual_acc_t_kernel(tc, vfs, p_lfs, n_lfs, W_hidden, b_hidden, 
             if n == 2:
                 nc.sync.dma_start(out=p_sb[:], in_=p_lfs.rearrange("(p t) d -> p (t d)", t=NT))
 
+        halves = (slice(0, CH // 2), slice(CH // 2, CH))
         for half in range(2):
             turn_words(wh_sb[:].bitcast(F32), "wh", half, half)
             copy_words("wh", half, nc.vector.tensor_copy)
-        nc.vector.quantize_mx(out=wh_codes[:].bitcast(FP8X4), scales=wh_scales[:], in_=g_of["wh"][:])
-        for half in range(2):
             turn_words(x_sb[0][:].bitcast(F32), 0, half, 2 + half)
             copy_words(0, half)
-        quantise_x(0)
+        for half in range(2):
+            quantise(g_of["wh"], wh_codes, wh_scales, halves[half])
+            quantise_x(0, halves[half])
 
         tz = bank(4, BF16)
         nc.tensor.transpose(tz[:, 0:P], zb[:], ident_b[:])
@@ -214,27 +230,29 @@ def tile_hypernymvisual_acc_t_kernel(tc, vfs, p_lfs, n_lfs, W_hidden, b_hidden, 
         g_we = keep.tile([P, EMB, 4], BF16, name="g_we", align_bytes=64)
         nc.vector.tensor_copy(out=g_we[:], in_=tb[:].rearrange("p (t d) -> p d t", t=4))
         nc.vector.quantize_mx(out=we_codes[:].bitcast(FP8X4), scales=we_scales[:], in_=g_we[:].rearrange("p d t -> p (d t)"))
-        for q in range(4):
-            hidden_mm(0, q, 6 + q % 2)
-            hidden_add(0, q)
-        quantise_h(0)
-        e_mm(0, 5)
-        e_copy(0)
         for half in range(2):
-            turn_words(x_sb[1][:].bitcast(F32), 1, half, half)
-            copy_words(1, half)
-        quantise_x(1)
+            for q in (2 * half, 2 * half + 1):
+                hidden_mm(0, q, 6 + q % 2)
+                hidden_add(0, q)
+            quantise_h(0, halves[half])
+            e_mm(0, 4 + half, halves[half])
+            e_copy(0, halves[half])
+        for n in range(1, EARLY):
+            for half in range(2):
+                turn_words(x_sb[n][:].bitcast(F32), n, half, 1 + (2 * n + half) % 3)
+                copy_words(n, half)
+            quantise_x(n)
 
         steps = []
         last_of = {}
         share = {}
         col = 0
         due = 0.0
-        for g, (width, many, part, want) in enumerate(GROUPS):
+        for g, (width, many, cuts, want) in enumerate(GROUPS):
             for s in range(0, NNEG, many):
-                due += want * many * width / part
-                share[len(steps)] = part if due >= 1.0 else 0
-                due -= 1.0 if due >= 1.0 else 0.0
+                due += want * many * width / P
+                share[len(steps)] = int(due)
+                due -= int(due)
                 steps.append((g, col, width, s, many))
             last_of[len(steps) - 1] = g
             col += width
@@ -258,12 +276,16 @@ def tile_hypernymvisual_acc_t_kernel(tc, vfs, p_lfs, n_lfs, W_hidden, b_hidden, 
 
         def square(k):
             g, col, width, s0, many = steps[k]
-            r = tiles[k]
-            cut = many * width - share[k]
+            blocks = many * width // P
+            cuts = GROUPS[g][2]
+            own = blocks - share[k]
+            edges = [i * own // cuts for i in range(cuts + 1)]
+            for a, b in zip(edges[:-1], edges[1:]):
+                part = tiles[k][:, a * P:b * P]
+                nc.scalar.activation(out=part, in_=part, func=ACT.Square)
             if share[k]:
-                nc.vector.tensor_tensor(out=r[:, cut:many * width], in0=r[:, cut:many * width], in1=r[:, cut:many * width], op=ALU.mult)
-            if cut:
-                nc.scalar.activation(out=r[:, 0:cut], in_=r[:, 0:cut], func=ACT.Square)
+                part = tiles[k][:, own * P:blocks * P]
+                nc.vector.tensor_tensor(out=part, in0=part, in1=part, op=ALU.mult)
 
         def add_up(k):
             g, col, width, s0, many = steps[k]
@@ -282,7 +304,7 @@ def tile_hypernymvisual_acc_t_kernel(tc, vfs, p_lfs, n_lfs, W_hidden, b_hidden, 
                     )
 
         def chunks_of(g):
-            first = sum(width for width, many, part, want in GROUPS[:g]) // CH
+            first = sum(width for width, many, cuts, want in GROUPS[:g]) // CH
             return first, first + GROUPS[g][0] // CH
 
         def roots(g):
@@ -293,9 +315,6 @@ def tile_hypernymvisual_acc_t_kernel(tc, vfs, p_lfs, n_lfs, W_hidden, b_hidden, 
                     in_=acc[g][c - first][:].rearrange("p (t j) -> p t j", t=TC),
                     func=ACT.Sqrt,
                 )
-
-        def root_pos():
-            nc.scalar.activation(out=sums[:, :, 0], in_=sums[:, :, 0], func=ACT.Sqrt)
 
         def negate(g):
             first, last = chunks_of(g)
@@ -316,25 +335,25 @@ def tile_hypernymvisual_acc_t_kernel(tc, vfs, p_lfs, n_lfs, W_hidden, b_hidden, 
         for n in range(NCH):
             o = FRONT[n]
             if n > 0:
-                for half in range(2 if n > 1 else 0):
+                for half in range(2 if n >= EARLY else 0):
                     at(o + 2 * half, lambda n, half: turn_words(x_sb[n][:].bitcast(F32), n, half, 5), n, half)
                     at(o + 2 * half + 1, copy_words, n, half)
-                if n > 1:
+                if n >= EARLY:
                     at(o + 5, quantise_x, n)
                 for q in range(4):
                     at(o + 6 + q, hidden_mm, n, q, 4 + 2 * (q % 2))
                     at(o + 7 + q, hidden_add, n, q)
                 at(o + 12, quantise_h, n)
                 at(o + 13, e_mm, n, 7)
-                at(o + 14, e_copy, n)
-            at(max(o + 15, 5), pos_turn, n, 7)
-            at(max(o + 16, 6), pos_diff, n)
-            at(max(o + 17, 7), pos_back, n, 7)
-            at(max(o + 18, 8), pos_sum, n)
-        at(FRONT_END + 1, root_pos)
+                at(o + 15, e_copy, n)
+            at(o + 16, pos_turn, n, 7)
+            at(o + 17, pos_diff, n)
+            at(o + 18, pos_square, n)
+            at(o + 19, pos_sum, n, 7)
+            at(o + 21, pos_root, n)
 
         with tc.manual_schedule():
-            for k in range(n_steps + LEAD + LAG_R + 6):
+            for k in range(n_steps + LEAD + LAG_R + 7):
                 if k < n_steps:
                     differences(k)
                 for what, args in extra.get(k, []):
@@ -344,7 +363,7 @@ def tile_hypernymvisual_acc_t_kernel(tc, vfs, p_lfs, n_lfs, W_hidden, b_hidden, 
                 b = k - LEAD
                 if 0 <= b < n_steps:
                     add_up(b)
-                for lag, what in ((LAG_R, roots), (LAG_R + 2, negate), (LAG_R + 3, store)):
+                for lag, what in ((LAG_R, roots), (LAG_R + 4, negate), (LAG_R + 5, store)):
                     if b - lag in last_of:
                         if what == roots or b - lag > FRONT_END:
                             what(last_of[b - lag])

@@ -21,11 +21,15 @@ NNEG = 128
 CH = 512
 NCH = B // CH
 TC = CH // P
-GROUPS = ((512, 2, 1, 0.19), (1536, 1, 2, 0.233), (2048, 1, 2, 0.243))
+GROUPS = (
+    (512, 2, 1024, 0.17, (0, 1, 2, 3)),
+    (1536, 1, 768, 0.235, (4, 5, 0, 1, 2, 3)),
+    (2048, 1, 1024, 0.245, (6, 7, 4, 5, 0, 1, 2, 3)),
+)
 WIDE = 2048
-LEAD = 6
-SQ = 3
-RBUFS = 8
+LEAD = 8
+SQ = 4
+RBUFS = 11
 LAG_R = 1
 EARLY = 4
 FRONT = (-13, -5, 9, 23, 44, 72, 100, 128)
@@ -248,11 +252,11 @@ def tile_hypernymvisual_acc_t_kernel(tc, vfs, p_lfs, n_lfs, W_hidden, b_hidden, 
         share = {}
         col = 0
         due = 0.0
-        for g, (width, many, cuts, want) in enumerate(GROUPS):
+        for g, (width, many, part, want, own_banks) in enumerate(GROUPS):
             for s in range(0, NNEG, many):
-                due += want * many * width / P
-                share[len(steps)] = int(due)
-                due -= int(due)
+                due += want * many * width / part
+                share[len(steps)] = part if due >= 1.0 else 0
+                due -= 1.0 if due >= 1.0 else 0.0
                 steps.append((g, col, width, s, many))
             last_of[len(steps) - 1] = g
             col += width
@@ -276,56 +280,57 @@ def tile_hypernymvisual_acc_t_kernel(tc, vfs, p_lfs, n_lfs, W_hidden, b_hidden, 
 
         def square(k):
             g, col, width, s0, many = steps[k]
-            blocks = many * width // P
-            cuts = GROUPS[g][2]
-            own = blocks - share[k]
-            edges = [i * own // cuts for i in range(cuts + 1)]
-            for a, b in zip(edges[:-1], edges[1:]):
-                part = tiles[k][:, a * P:b * P]
-                nc.scalar.activation(out=part, in_=part, func=ACT.Square)
+            cut = many * width - share[k]
             if share[k]:
-                part = tiles[k][:, own * P:blocks * P]
+                part = tiles[k][:, cut:many * width]
                 nc.vector.tensor_tensor(out=part, in0=part, in1=part, op=ALU.mult)
+            if cut:
+                nc.scalar.activation(out=tiles[k][:, 0:cut], in_=tiles[k][:, 0:cut], func=ACT.Square)
 
         def add_up(k):
             g, col, width, s0, many = steps[k]
             if s0 == 0:
-                acc[g] = [bank(b) for b in range(col // CH, (col + width) // CH)]
+                acc[g] = [bank(b) for b in GROUPS[g][4]]
+            nb = len(acc[g])
+            rounds = width // P // nb
             for i in range(many):
                 s = s0 + i
                 for t in range(width // P):
                     nc.tensor.matmul(
-                        out=acc[g][t // TC][:, t % TC * P:(t % TC + 1) * P],
+                        out=acc[g][t % nb][:, t // nb * P:(t // nb + 1) * P],
                         lhsT=tiles[k][:, i * width + t * P:i * width + (t + 1) * P],
                         rhs=ident[:, P - s:2 * P - s],
                         is_transpose=True,
-                        start=(s == 0 and t % TC == 0),
-                        stop=(s == NNEG - 1 and t % TC == TC - 1),
+                        start=(s == 0 and t // nb == 0),
+                        stop=(s == NNEG - 1 and t // nb == rounds - 1),
                     )
 
-        def chunks_of(g):
-            first = sum(width for width, many, cuts, want in GROUPS[:g]) // CH
-            return first, first + GROUPS[g][0] // CH
+        def group_tiles(g):
+            first = sum(group[0] for group in GROUPS[:g]) // P
+            return first, GROUPS[g][0] // P
 
         def roots(g):
-            first, last = chunks_of(g)
-            for c in range(first, last):
+            first, n_tiles = group_tiles(g)
+            nb = len(acc[g])
+            for b in range(nb):
                 nc.scalar.activation(
-                    out=sums[:, c * TC:(c + 1) * TC, 1:NNEG + 1],
-                    in_=acc[g][c - first][:].rearrange("p (t j) -> p t j", t=TC),
+                    out=sums[:, first + b:first + n_tiles:nb, 1:NNEG + 1],
+                    in_=acc[g][b][:, 0:n_tiles // nb * P].rearrange("p (t j) -> p t j", j=P),
                     func=ACT.Sqrt,
                 )
 
+        def pieces(g):
+            first, n_tiles = group_tiles(g)
+            chunks = [slice(t, t + TC) for t in range(first, first + n_tiles, TC)]
+            return chunks[0::2] + chunks[1::2]
+
         def negate(g):
-            first, last = chunks_of(g)
-            for c in range(first, last):
-                part = sums[:, c * TC:(c + 1) * TC, :]
-                nc.vector.tensor_scalar(out=part, in0=part, scalar1=-1.0, scalar2=None, op0=ALU.mult)
+            for t in pieces(g):
+                nc.vector.tensor_scalar(out=sums[:, t, :], in0=sums[:, t, :], scalar1=-1.0, scalar2=None, op0=ALU.mult)
 
         def store(g):
-            first, last = chunks_of(g)
-            for c in range(first, last):
-                nc.sync.dma_start(out=out_view[:, c * TC:(c + 1) * TC, :], in_=sums[:, c * TC:(c + 1) * TC, :])
+            for t in pieces(g):
+                nc.sync.dma_start(out=out_view[:, t, :], in_=sums[:, t, :])
 
         extra = {}
 
@@ -336,20 +341,20 @@ def tile_hypernymvisual_acc_t_kernel(tc, vfs, p_lfs, n_lfs, W_hidden, b_hidden, 
             o = FRONT[n]
             if n > 0:
                 for half in range(2 if n >= EARLY else 0):
-                    at(o + 2 * half, lambda n, half: turn_words(x_sb[n][:].bitcast(F32), n, half, 5), n, half)
+                    at(o + 2 * half, lambda n, half: turn_words(x_sb[n][:].bitcast(F32), n, half, 6), n, half)
                     at(o + 2 * half + 1, copy_words, n, half)
                 if n >= EARLY:
                     at(o + 5, quantise_x, n)
                 for q in range(4):
-                    at(o + 6 + q, hidden_mm, n, q, 4 + 2 * (q % 2))
+                    at(o + 6 + q, hidden_mm, n, q, 6 + q % 2)
                     at(o + 7 + q, hidden_add, n, q)
                 at(o + 12, quantise_h, n)
-                at(o + 13, e_mm, n, 7)
+                at(o + 13, e_mm, n, 5 if n < EARLY else 7)
                 at(o + 15, e_copy, n)
-            at(o + 16, pos_turn, n, 7)
+            at(o + 16, pos_turn, n, 5 if n < EARLY else 7)
             at(o + 17, pos_diff, n)
             at(o + 18, pos_square, n)
-            at(o + 19, pos_sum, n, 7)
+            at(o + 19, pos_sum, n, 5 if n < EARLY else 7)
             at(o + 21, pos_root, n)
 
         with tc.manual_schedule():

from contextlib import ExitStack

import concourse.masks as masks
import concourse.mybir as mybir

F32 = mybir.dt.float32
BF16 = mybir.dt.bfloat16
U32 = mybir.dt.uint32
U8 = mybir.dt.uint8
FP8X4 = mybir.dt.float8_e4m3fn_x4
ALU = mybir.AluOpType
ACT = mybir.ActivationFunctionType

P = 128
B = 4096
NT = B // P
VF = 512
HID = 512
EMB = 128
NNEG = 128
CH = 512
NCH = B // CH
TC = CH // P
GROUPS = (
    (512, 2, 1024, 0.17, (0, 1, 2, 3)),
    (1536, 1, 768, 0.235, (4, 5, 0, 1, 2, 3)),
    (2048, 1, 1024, 0.245, (6, 7, 4, 5, 0, 1, 2, 3)),
)
WIDE = 2048
LEAD = 8
SQ = 4
RBUFS = 11
LAG_R = 1
EARLY = 4
FRONT = (-13, -5, 9, 23, 44, 72, 100, 128)
FRONT_END = FRONT[-1] + 23

FLOPS = 2 * B * VF * HID + 2 * B * HID * EMB + 4 * B * (NNEG + 1) * EMB


def tile_hypernymvisual_acc_t_kernel(tc, vfs, p_lfs, n_lfs, W_hidden, b_hidden, W_embed, b_embed, out):
    nc = tc.nc
    out_flat = out.rearrange("a b -> (a b)")
    out_view = out.rearrange("(p t) c -> p t c", t=NT)
    with ExitStack() as ctx:
        keep = ctx.enter_context(tc.tile_pool(name="keep", bufs=1))
        stg = ctx.enter_context(tc.tile_pool(name="stage", bufs=2))
        rpool = ctx.enter_context(tc.tile_pool(name="rpool", bufs=RBUFS))
        banks = ctx.enter_context(tc.psum_pool(name="banks", bufs=1))

        def bank(i, dtype=F32):
            return banks.tile([P, CH], dtype, name="b%d" % i, tag="b%d" % i)

        wh_sb = keep.tile([P, 4 * VF], BF16, name="wh_sb")
        x_view = vfs.rearrange("(p t) k -> p (t k)", t=NT)
        x_sb = {}

        def load_x(n):
            x = keep.tile([P, TC * VF], BF16, name="x%d" % n)
            nc.sync.dma_start(out=x[:], in_=x_view[:, n * TC * VF:(n + 1) * TC * VF])
            x_sb[n] = x

        x_sb[0] = keep.tile([P, TC * VF], BF16, name="x0")
        for half in range(2):
            rows = slice(half * 2 * VF, (half + 1) * 2 * VF)
            nc.sync.dma_start(
                out=wh_sb[:, rows].rearrange("p (m k) -> p m k", m=2),
                in_=W_hidden[half * 2 * P:(half + 1) * 2 * P, :].rearrange("(m p) k -> p m k", p=P),
            )
            nc.sync.dma_start(out=x_sb[0][:, rows], in_=x_view[:, rows])
        n_sb = keep.tile([P, EMB], BF16, name="n_sb")
        nc.sync.dma_start(out=n_sb[:], in_=n_lfs)
        we_sb = keep.tile([P, HID], BF16, name="we_sb")
        nc.sync.dma_start(out=we_sb[:], in_=W_embed)
        zb = keep.tile([P, P], BF16, name="zb")
        nc.vector.memset(zb[:], 0.0)
        nc.sync.dma_start(out=zb[0:4, :], in_=b_hidden.rearrange("(m p) -> m p", p=P))
        nc.sync.dma_start(out=zb[4:5, :], in_=b_embed.rearrange("(o p) -> o p", o=1))
        load_x(1)

        ident = keep.tile([P, 2 * P], F32, name="ident")
        masks.make_identity(nc, ident[:, P:2 * P])
        nc.vector.tensor_copy(out=ident[:, 0:P], in_=ident[:, P:2 * P])
        ident_f = ident[:, P:2 * P]
        ident_b = keep.tile([P, P], BF16, name="ident_b")
        masks.make_identity(nc, ident_b[:])
        n_two = keep.tile([P, 2, NNEG], F32, name="n_two")
        n_tab = keep.tile([P, NNEG], F32, name="n_tab")
        sums = keep.tile([P, NT, NNEG + 1], F32, name="sums")
        eT = keep.tile([P, B], F32, name="eT")
        bias = keep.tile([P, 8], F32, name="bias")
        warm = keep.tile([P, 2], F32, name="warm")
        nc.vector.memset(warm[:], 1.0)
        nc.scalar.activation(out=warm[:, 1:2], in_=warm[:, 0:1], func=ACT.Sqrt)
        ones = keep.tile([P, 2], F32, name="ones")
        nc.vector.memset(ones[:], 1.0)
        wh_codes = keep.tile([P, HID], U32, name="wh_codes", align_bytes=64)
        wh_scales = keep.tile([P, HID], U8, name="wh_scales", align_bytes=64)
        we_codes = keep.tile([P, EMB], U32, name="we_codes", align_bytes=64)
        we_scales = keep.tile([P, EMB], U8, name="we_scales", align_bytes=64)
        g_of = {}
        x_q = {}
        h_q = {}
        g2_of = {}
        held = {}

        def turn_words(words, key, half, b):
            if half == 0:
                g_of[key] = stg.tile([P, 4 * CH], BF16, name="g", tag="g", bufs=5, align_bytes=64)
            tp = bank(b)
            for tt in range(2):
                for u in range(2):
                    blk = (2 * half + tt) * 256 + 128 * u
                    nc.tensor.transpose(tp[:, (2 * tt + u) * P:(2 * tt + u + 1) * P], words[:, blk:blk + P], ident_f)
            held[(key, half)] = tp

        def copy_words(key, half, copy=nc.scalar.copy):
            dst = g_of[key][:].bitcast(F32)[:, half * CH:(half + 1) * CH].rearrange("q (tt c u) -> q tt c u", tt=2, u=2)
            copy(out=dst, in_=held[(key, half)][:].rearrange("q (tt u c) -> q tt c u", tt=2, u=2))

        def quantise(src, codes, scales, cols):
            nc.vector.quantize_mx(out=codes[:, cols].bitcast(FP8X4), scales=scales[:, cols], in_=src[:, 4 * cols.start:4 * cols.stop])

        def quantise_x(n, cols=slice(0, CH)):
            if cols.start == 0:
                x_codes = stg.tile([P, CH], U32, name="x_codes", tag="x_codes", bufs=4, align_bytes=64)
                x_scales = stg.tile([P, CH], U8, name="x_scales", tag="x_scales", bufs=4, align_bytes=64)
                x_q[n] = (x_codes, x_scales)
            quantise(g_of[n], x_q[n][0], x_q[n][1], cols)

        def hidden_mm(n, q, b):
            x_codes, x_scales = x_q[n]
            ph = bank(b)
            for t in range(4):
                nc.tensor.matmul_mx(
                    out=ph[:, t * P:(t + 1) * P],
                    lhsT=wh_codes[:, t * P:(t + 1) * P].bitcast(FP8X4),
                    lhsT_scale=wh_scales[:, t * P:(t + 1) * P],
                    rhs=x_codes[:, q * P:(q + 1) * P].bitcast(FP8X4),
                    rhs_scale=x_scales[:, q * P:(q + 1) * P],
                    start=True,
                    stop=True,
                )
            held[("ph", n, q)] = ph

        def hidden_add(n, q):
            if q == 0:
                g2_of[n] = stg.tile([P, CH, 4], BF16, name="g2", tag="g2", align_bytes=64)
            nc.vector.tensor_tensor(
                out=g2_of[n][:, q * P:(q + 1) * P, :],
                in0=held[("ph", n, q)][:].rearrange("p (t c) -> p c t", t=4),
                in1=bias[:, 0:4].unsqueeze(1).to_broadcast([P, P, 4]),
                op=ALU.add,
            )

        def quantise_h(n, cols=slice(0, CH)):
            if cols.start == 0:
                h_codes = stg.tile([P, CH], U32, name="h_codes", tag="h_codes", align_bytes=64)
                h_scales = stg.tile([P, CH], U8, name="h_scales", tag="h_scales", align_bytes=64)
                h_q[n] = (h_codes, h_scales)
            quantise(g2_of[n][:].rearrange("p c t -> p (c t)"), h_q[n][0], h_q[n][1], cols)

        def e_mm(n, b, cols=slice(0, CH)):
            h_codes, h_scales = h_q[n]
            pe = bank(b)
            nc.tensor.matmul_mx(
                out=pe[:, cols],
                lhsT=we_codes[:].bitcast(FP8X4),
                lhsT_scale=we_scales[:],
                rhs=h_codes[:, cols].bitcast(FP8X4),
                rhs_scale=h_scales[:, cols],
                start=True,
                stop=True,
            )
            held[("e", n)] = pe

        def e_copy(n, cols=slice(0, CH)):
            nc.scalar.activation(out=eT[:, n * CH + cols.start:n * CH + cols.stop], in_=held[("e", n)][:, cols], func=ACT.Identity, bias=bias[:, 4:5])

        def pos_turn(n, b):
            tq = bank(b, BF16)
            for s in range(TC):
                t = TC * n + s
                nc.tensor.transpose(tq[:, s * P:(s + 1) * P], p_sb[:, t * EMB:(t + 1) * EMB], ident_b[:])
            held[("tq", n)] = tq

        def pos_diff(n):
            rp = stg.tile([P, CH], F32, name="rp", tag="rp")
            nc.vector.tensor_tensor(out=rp[:], in0=eT[:, n * CH:(n + 1) * CH], in1=held[("tq", n)][:], op=ALU.subtract)
            held[("rp", n)] = rp

        def pos_square(n):
            rp = held[("rp", n)]
            nc.vector.scalar_tensor_tensor(out=rp[:], in0=rp[:], scalar=0.0, in1=rp[:], op0=ALU.min, op1=ALU.mult)

        def pos_sum(n, b):
            tr = bank(b)
            for s in range(TC):
                nc.tensor.matmul(out=tr[:, s:s + 1], lhsT=held[("rp", n)][:, s * P:(s + 1) * P], rhs=ones[:, 0:1], start=True, stop=True)
            held[("tr", n)] = tr

        def pos_root(n):
            nc.scalar.activation(out=sums[:, TC * n:TC * (n + 1), 0], in_=held[("tr", n)][:, 0:TC], func=ACT.Sqrt)

        tn = bank(4, BF16)
        nc.tensor.transpose(tn[:, 0:P], n_sb[:], ident_b[:])
        for i in range(2):
            nc.vector.tensor_copy(out=n_two[:, i, :], in_=tn[:, 0:P])
        nc.sync.dma_start(out=out_flat[0:P * 2 * NNEG].rearrange("(d c) -> d c", c=2 * NNEG), in_=n_two[:].rearrange("p i j -> p (i j)"))
        nc.sync.dma_start(out=n_tab[:], in_=out_flat[0:P * (2 * NNEG + 1)].rearrange("(d c) -> d c", c=2 * NNEG + 1)[:, 0:NNEG])
        p_sb = keep.tile([P, NT * EMB], BF16, name="p_sb")
        for n in range(2, NCH):
            load_x(n)
            if n == 2:
                nc.sync.dma_start(out=p_sb[:], in_=p_lfs.rearrange("(p t) d -> p (t d)", t=NT))

        halves = (slice(0, CH // 2), slice(CH // 2, CH))
        for half in range(2):
            turn_words(wh_sb[:].bitcast(F32), "wh", half, half)
            copy_words("wh", half, nc.vector.tensor_copy)
            turn_words(x_sb[0][:].bitcast(F32), 0, half, 2 + half)
            copy_words(0, half)
        for half in range(2):
            quantise(g_of["wh"], wh_codes, wh_scales, halves[half])
            quantise_x(0, halves[half])

        tz = bank(4, BF16)
        nc.tensor.transpose(tz[:, 0:P], zb[:], ident_b[:])
        nc.vector.tensor_copy(out=bias[:, 0:5], in_=tz[:, 0:5])

        tb = bank(5, BF16)
        for t in range(4):
            nc.tensor.transpose(tb[:, t * P:(t + 1) * P], we_sb[:, t * P:(t + 1) * P], ident_b[:])
        g_we = keep.tile([P, EMB, 4], BF16, name="g_we", align_bytes=64)
        nc.vector.tensor_copy(out=g_we[:], in_=tb[:].rearrange("p (t d) -> p d t", t=4))
        nc.vector.quantize_mx(out=we_codes[:].bitcast(FP8X4), scales=we_scales[:], in_=g_we[:].rearrange("p d t -> p (d t)"))
        for half in range(2):
            for q in (2 * half, 2 * half + 1):
                hidden_mm(0, q, 6 + q % 2)
                hidden_add(0, q)
            quantise_h(0, halves[half])
            e_mm(0, 4 + half, halves[half])
            e_copy(0, halves[half])
        for n in range(1, EARLY):
            for half in range(2):
                turn_words(x_sb[n][:].bitcast(F32), n, half, 1 + (2 * n + half) % 3)
                copy_words(n, half)
            quantise_x(n)

        steps = []
        last_of = {}
        share = {}
        col = 0
        due = 0.0
        for g, (width, many, part, want, own_banks) in enumerate(GROUPS):
            for s in range(0, NNEG, many):
                due += want * many * width / part
                share[len(steps)] = part if due >= 1.0 else 0
                due -= 1.0 if due >= 1.0 else 0.0
                steps.append((g, col, width, s, many))
            last_of[len(steps) - 1] = g
            col += width
        n_steps = len(steps)
        tiles = {}
        acc = {}

        def differences(k):
            g, col, width, s0, many = steps[k]
            r = rpool.tile([P, WIDE], F32, name="r", tag="r")
            for i in range(many):
                nc.vector.tensor_scalar(
                    out=r[:, i * width:(i + 1) * width],
                    in0=eT[:, col:col + width],
                    scalar1=n_tab[:, s0 + i:s0 + i + 1],
                    scalar2=0.0,
                    op0=ALU.subtract,
                    op1=ALU.min,
                )
            tiles[k] = r

        def square(k):
            g, col, width, s0, many = steps[k]
            cut = many * width - share[k]
            if share[k]:
                part = tiles[k][:, cut:many * width]
                nc.vector.tensor_tensor(out=part, in0=part, in1=part, op=ALU.mult)
            if cut:
                nc.scalar.activation(out=tiles[k][:, 0:cut], in_=tiles[k][:, 0:cut], func=ACT.Square)

        def add_up(k):
            g, col, width, s0, many = steps[k]
            if s0 == 0:
                acc[g] = [bank(b) for b in GROUPS[g][4]]
            nb = len(acc[g])
            rounds = width // P // nb
            for i in range(many):
                s = s0 + i
                for t in range(width // P):
                    nc.tensor.matmul(
                        out=acc[g][t % nb][:, t // nb * P:(t // nb + 1) * P],
                        lhsT=tiles[k][:, i * width + t * P:i * width + (t + 1) * P],
                        rhs=ident[:, P - s:2 * P - s],
                        is_transpose=True,
                        start=(s == 0 and t // nb == 0),
                        stop=(s == NNEG - 1 and t // nb == rounds - 1),
                    )

        def group_tiles(g):
            first = sum(group[0] for group in GROUPS[:g]) // P
            return first, GROUPS[g][0] // P

        def roots(g):
            first, n_tiles = group_tiles(g)
            nb = len(acc[g])
            for b in range(nb):
                nc.scalar.activation(
                    out=sums[:, first + b:first + n_tiles:nb, 1:NNEG + 1],
                    in_=acc[g][b][:, 0:n_tiles // nb * P].rearrange("p (t j) -> p t j", j=P),
                    func=ACT.Sqrt,
                )

        def pieces(g):
            first, n_tiles = group_tiles(g)
            chunks = [slice(t, t + TC) for t in range(first, first + n_tiles, TC)]
            return chunks[0::2] + chunks[1::2]

        def negate(g):
            for t in pieces(g):
                nc.vector.tensor_scalar(out=sums[:, t, :], in0=sums[:, t, :], scalar1=-1.0, scalar2=None, op0=ALU.mult)

        def store(g):
            for t in pieces(g):
                nc.sync.dma_start(out=out_view[:, t, :], in_=sums[:, t, :])

        extra = {}

        def at(k, what, *args):
            extra.setdefault(k, []).append((what, args))

        for n in range(NCH):
            o = FRONT[n]
            if n > 0:
                for half in range(2 if n >= EARLY else 0):
                    at(o + 2 * half, lambda n, half: turn_words(x_sb[n][:].bitcast(F32), n, half, 6), n, half)
                    at(o + 2 * half + 1, copy_words, n, half)
                if n >= EARLY:
                    at(o + 5, quantise_x, n)
                for q in range(4):
                    at(o + 6 + q, hidden_mm, n, q, 6 + q % 2)
                    at(o + 7 + q, hidden_add, n, q)
                at(o + 12, quantise_h, n)
                at(o + 13, e_mm, n, 5 if n < EARLY else 7)
                at(o + 15, e_copy, n)
            at(o + 16, pos_turn, n, 5 if n < EARLY else 7)
            at(o + 17, pos_diff, n)
            at(o + 18, pos_square, n)
            at(o + 19, pos_sum, n, 5 if n < EARLY else 7)
            at(o + 21, pos_root, n)

        with tc.manual_schedule():
            for k in range(n_steps + LEAD + LAG_R + 7):
                if k < n_steps:
                    differences(k)
                for what, args in extra.get(k, []):
                    what(*args)
                if 0 <= k - SQ < n_steps:
                    square(k - SQ)
                b = k - LEAD
                if 0 <= b < n_steps:
                    add_up(b)
                for lag, what in ((LAG_R, roots), (LAG_R + 4, negate), (LAG_R + 5, store)):
                    if b - lag in last_of:
                        if what == roots or b - lag > FRONT_END:
                            what(last_of[b - lag])
                        else:
                            at(max(k + 1, FRONT_END + 3), what, last_of[b - lag])
